import numpy as np
import ml_dtypes


def mxq(x, axis, fmt="e4m3"):
    dtype, down = {"e4m3": (ml_dtypes.float8_e4m3fn, 7), "e5m2": (ml_dtypes.float8_e5m2, 14)}[fmt]
    v = np.moveaxis(np.asarray(x, np.float32).astype(ml_dtypes.bfloat16).astype(np.float64), axis, -1)
    blocks = v.reshape(v.shape[:-1] + (-1, 32))
    amax = np.abs(blocks).max(-1, keepdims=True)
    byte = np.maximum(np.where(amax > 0, np.frexp(amax)[1] - 1 + 127, 0) - down, 1)
    scale = np.exp2(byte - 127.0)
    codes = (blocks / scale).astype(np.float32).astype(dtype).astype(np.float64)
    return np.moveaxis((codes * scale).reshape(v.shape), -1, axis)


WIDE = False


def mx_kscale(k):
    if not WIDE:
        return np.ones(k)
    levels = np.array([10, -10, 5, -5, 0])
    if k % 512:
        return np.exp2(np.random.permutation(np.resize(levels, k // 32))).repeat(32)
    a = np.empty((k // 512, 16))
    for p in range(k // 512):
        a[p, :8] = np.random.permutation(np.resize(levels, 8))
        for g in range(8):
            far = levels[np.abs(levels - a[p, g]) >= 10]
            a[p, g + 8] = far[np.random.randint(len(far))]
    return np.exp2(a.ravel()).repeat(32)


BF16 = ml_dtypes.bfloat16


def bf(x):
    return np.asarray(x, np.float32).astype(BF16)


def f64(x):
    return np.asarray(x).astype(np.float64)


B, S, D, QC, KVC, FF = 2, 2048, 1024, 16, 2, 4096
HD = D // QC
REP = QC // KVC
KV = KVC * HD
EPS = 1e-5


def rotate_every_two(u):
    u1 = u[..., ::2]
    u2 = u[..., 1::2]
    return np.stack((-u2, u1), axis=-1).reshape(*u.shape[:-1], -1)


def apply_rope(u, sin, cos):
    return u * cos + rotate_every_two(u) * sin


def rmsnorm(u, w):
    return u / np.sqrt(np.square(u).mean(-1, keepdims=True) + EPS) * w


def setup_inputs():
    s = mx_kscale(D)
    pos = np.arange(S, dtype=np.float64)
    inv_freq = 1.0 / (10000.0 ** (np.arange(0, HD, 2, dtype=np.float64) / HD))
    freqs = pos[:, None] * inv_freq[None, :]
    return {"x": bf(np.random.standard_normal((B, S, D))),
            "norm1_w": bf((1.0 + 0.1 * np.random.standard_normal(D)) * s),
            "wqkv": bf(np.random.standard_normal((D, D + 2 * KV)) * 1.5 / np.sqrt(D) / s[:, None]),
            "rope_sin": bf(np.repeat(np.sin(freqs), 2, axis=-1)),
            "rope_cos": bf(np.repeat(np.cos(freqs), 2, axis=-1))}


def reference(x, norm1_w, wqkv, rope_sin, rope_cos):
    sin = f64(rope_sin)[:S]
    cos = f64(rope_cos)[:S]
    xn = rmsnorm(f64(x), f64(norm1_w))
    qkv = mxq(xn, 2, "e4m3") @ mxq(f64(wqkv), 0, "e4m3")
    q = np.moveaxis(qkv[..., :D].reshape(B, S, REP, KVC, HD), 1, 3)
    q = apply_rope(q, sin, cos)
    k, v = np.split(qkv[..., D:], 2, axis=-1)
    k = k.reshape(B, S, KVC, HD).swapaxes(1, 2)
    v = v.reshape(B, S, KVC, HD).swapaxes(1, 2)
    k = apply_rope(k, sin, cos) * HD ** -0.5
    return q, k, v

@@ -1,0 +1,258 @@
+from contextlib import ExitStack
+
+import concourse.mybir as mybir
+from concourse.masks import make_identity
+
+F32 = mybir.dt.float32
+BF16 = mybir.dt.bfloat16
+U32 = mybir.dt.uint32
+U8 = mybir.dt.uint8
+FP8X4 = mybir.dt.float8_e4m3fn_x4
+ALU = mybir.AluOpType
+ACT = mybir.ActivationFunctionType
+
+P = 128
+BATCH = 2
+SEQ = 2048
+D = 1024
+HD = 64
+HALF = HD // 2
+Q_HEADS = 16
+KV_HEADS = 2
+ROPED_HEADS = Q_HEADS + KV_HEADS
+HEADS = Q_HEADS + 2 * KV_HEADS
+N_OUT = HEADS * HD
+EPS = 1e-5
+
+PACK = 4
+K_PASS = P * PACK
+PASSES = D // K_PASS
+PAIRS = PACK // 2
+
+TOK = SEQ // P
+CHUNK = 4
+TILES = BATCH * TOK
+CHUNKS = TILES // CHUNK
+BANK = 512
+BANK_HEADS = BANK // HD
+
+FLOPS = 2 * BATCH * SEQ * D * N_OUT
+
+
+def tile_block_pa_t_kernel(
+    tc, x, norm1_w, wqkv, rope_sin, rope_cos, out_0, out_1, out_2
+):
+    nc = tc.nc
+
+    x_view = x.rearrange("b (p t) k -> b p t k", t=TOK)
+    q_view = out_0.rearrange("b r g (p t) d -> b p (r g) t d", t=TOK)
+    k_view = out_1.rearrange("b g (p t) d -> b p g t d", t=TOK)
+    v_view = out_2.rearrange("b g (p t) d -> b p g t d", t=TOK)
+
+    with ExitStack() as ctx:
+        const = ctx.enter_context(tc.tile_pool(name="const", bufs=1))
+        x_pool = ctx.enter_context(tc.tile_pool(name="x_pool", bufs=4))
+        stat = ctx.enter_context(tc.tile_pool(name="stat", bufs=3))
+        work = ctx.enter_context(tc.tile_pool(name="work", bufs=3))
+        out_pool = ctx.enter_context(tc.tile_pool(name="out_pool", bufs=3))
+        xt_psum = ctx.enter_context(tc.psum_pool(name="xt_psum", bufs=2))
+        acc_psum = ctx.enter_context(tc.psum_pool(name="acc_psum", bufs=2))
+
+        x_tiles = {}
+        rstd_tiles = {}
+        grouped_tiles = {}
+        acc_tiles = {}
+        out_tiles = {}
+
+        def load_x(chunk):
+            b, t0 = divmod(chunk * CHUNK, TOK)
+            x_sb = x_pool.tile([P, CHUNK, D], BF16)
+            nc.sync.dma_start(out=x_sb[:], in_=x_view[b, :, t0 : t0 + CHUNK, :])
+            x_tiles[chunk] = x_sb
+
+        load_x(0)
+        gain = const.tile([P, D], BF16)
+        nc.scalar.dma_start(out=gain[:], in_=norm1_w.partition_broadcast(P))
+        w_raw = const.tile([P, PASSES, PACK, N_OUT], BF16)
+        w_rows = wqkv.rearrange("(c p j) n -> p c j n", p=P, j=PACK)
+        for c in range(PASSES):
+            nc.sync.dma_start(out=w_raw[:, c, :, :], in_=w_rows[:, c, :, :])
+        cos_raw = const.tile([P, TOK, HD], BF16)
+        nc.sync.dma_start(out=cos_raw[:], in_=rope_cos.rearrange("(p t) d -> p t d", t=TOK))
+        sin_raw = const.tile([P, TOK, HD], BF16)
+        nc.sync.dma_start(out=sin_raw[:], in_=rope_sin.rearrange("(p t) d -> p t d", t=TOK))
+        for chunk in range(1, 4):
+            load_x(chunk)
+
+        eps = const.tile([P, 1], F32)
+        nc.vector.memset(eps[:], EPS)
+        warm = const.tile([P, 1], F32)
+        nc.scalar.activation(out=warm[:], in_=eps[:], func=ACT.Sqrt)
+        ident = const.tile([P, P], F32)
+        make_identity(nc, ident[:])
+
+        sin_pairs = sin_raw[:].rearrange("p t (i e) -> p t e i", e=2)
+        sin_q = const.tile([P, TOK, 2, HALF], F32)
+        sin_k = const.tile([P, TOK, 2, HALF], F32)
+        cos_k = const.tile([P, TOK, HD], F32)
+        k_scale = HD**-0.5
+        for table, scale in ((sin_q, 1.0), (sin_k, k_scale)):
+            for e, sign in ((0, -1.0), (1, 1.0)):
+                nc.gpsimd.tensor_scalar(
+                    out=table[:, :, e, :],
+                    in0=sin_pairs[:, :, e, :],
+                    scalar1=sign * scale,
+                    scalar2=0.0,
+                    op0=ALU.mult,
+                    op1=ALU.add,
+                )
+        nc.gpsimd.tensor_scalar(
+            out=cos_k[:], in0=cos_raw[:], scalar1=k_scale, scalar2=0.0, op0=ALU.mult, op1=ALU.add
+        )
+
+        w_grouped = const.tile([P, PASSES, N_OUT, PACK], BF16, align_bytes=64)
+        w_codes = const.tile([P, PASSES, N_OUT], U32, align_bytes=64)
+        w_scales = const.tile([P, PASSES, N_OUT], U8, align_bytes=64)
+        for c in range(PASSES):
+            src = w_raw[:, c, :, :].rearrange("p j (m i) -> p m j i", i=4)
+            dst = w_grouped[:, c, :, :].rearrange("p (m i) j -> p m j i", i=4)
+            if c == 0:
+                nc.vector.tensor_copy(out=dst, in_=src)
+            else:
+                nc.scalar.copy(out=dst, in_=src)
+        for c in range(PASSES):
+            for n0, n1 in ((0, 1024), (1024, N_OUT)):
+                nc.vector.quantize_mx(
+                    out=w_codes[:, c, n0:n1].bitcast(FP8X4),
+                    scales=w_scales[:, c, n0:n1],
+                    in_=w_grouped[:, c, n0:n1, :].rearrange("p n j -> p (n j)"),
+                )
+
+        def statistics(chunk):
+            x_sb = x_tiles[chunk]
+            sum_sq = stat.tile([P, CHUNK], F32)
+            for j in range(CHUNK):
+                squares = work.tile([P, D], BF16)
+                nc.scalar.activation(
+                    out=squares[:], in_=x_sb[:, j, :], func=ACT.Square,
+                    accum_out=sum_sq[:, j : j + 1],
+                )
+            rms = stat.tile([P, CHUNK], F32)
+            nc.scalar.activation(out=rms[:], in_=sum_sq[:], func=ACT.Sqrt, bias=eps[:], scale=1.0 / D)
+            rstd = stat.tile([P, CHUNK], F32)
+            nc.vector.reciprocal(out=rstd[:], in_=rms[:])
+            rstd_tiles[chunk] = rstd
+
+        def normalise_and_transpose(n):
+            chunk, j = divmod(n, CHUNK)
+            xn = work.tile([P, D], BF16)
+            nc.vector.scalar_tensor_tensor(
+                out=xn[:], in0=x_tiles[chunk][:, j, :], scalar=rstd_tiles[chunk][:, j : j + 1],
+                in1=gain[:], op0=ALU.mult, op1=ALU.mult,
+            )
+            pairs = xn[:].bitcast(F32)
+            xt = xt_psum.tile([P, PASSES, PAIRS, P], F32)
+            for c in range(PASSES):
+                for u in range(PAIRS):
+                    first = c * P * PAIRS + u
+                    nc.tensor.transpose(
+                        xt[:, c, u, :], pairs[:, first : (c + 1) * P * PAIRS : PAIRS], ident[:]
+                    )
+            grouped = work.tile([P, PASSES, P, PACK], BF16, align_bytes=64)
+            nc.scalar.copy(
+                out=grouped[:].rearrange("p c r j -> p (c r j)").bitcast(F32),
+                in_=xt[:].rearrange("p c u r -> p c r u"),
+            )
+            grouped_tiles[n] = grouped
+
+        def quantise_and_multiply(n):
+            codes = work.tile([P, PASSES, P], U32, align_bytes=64)
+            scales = work.tile([P, PASSES, P], U8, align_bytes=64)
+            nc.vector.quantize_mx(
+                out=codes[:].rearrange("p c r -> p (c r)").bitcast(FP8X4),
+                scales=scales[:].rearrange("p c r -> p (c r)"),
+                in_=grouped_tiles.pop(n)[:].rearrange("p c r j -> p (c r j)"),
+            )
+            acc_q0 = acc_psum.tile([P, BANK], F32)
+            acc_q1 = acc_psum.tile([P, BANK], F32)
+            acc_kv = acc_psum.tile([P, 2 * KV_HEADS * HD], F32)
+            n0 = 0
+            for acc in (acc_q0, acc_q1, acc_kv):
+                width = acc.shape[1]
+                for c in range(PASSES):
+                    nc.tensor.matmul_mx(
+                        out=acc[:],
+                        lhsT=codes[:, c, :].bitcast(FP8X4),
+                        lhsT_scale=scales[:, c, :],
+                        rhs=w_codes[:, c, n0 : n0 + width].bitcast(FP8X4),
+                        rhs_scale=w_scales[:, c, n0 : n0 + width],
+                        start=(c == 0),
+                        stop=(c == PASSES - 1),
+                    )
+                n0 += width
+            acc_tiles[n] = (acc_q0, acc_q1, acc_kv)
+
+        def rope_products(u, heads, cos_row, sin_rows, straight, cross):
+            nc.vector.tensor_tensor(
+                out=straight,
+                in0=u.rearrange("p (h d) -> p h d", d=HD),
+                in1=cos_row.unsqueeze(1).to_broadcast([P, heads, HD]),
+                op=ALU.mult,
+            )
+            partners = u.rearrange("p (h i e) -> p e h i", i=HALF, e=2)[:, ::-1, :, :]
+            nc.vector.tensor_tensor(
+                out=cross,
+                in0=partners,
+                in1=sin_rows.unsqueeze(2).to_broadcast([P, 2, heads, HALF]),
+                op=ALU.mult,
+            )
+
+        def rope_and_store(n):
+            chunk, j = divmod(n, CHUNK)
+            b, t0 = divmod(chunk * CHUNK, TOK)
+            t = t0 + j
+            if j == 0:
+                out_sb = out_pool.tile([P, HEADS, CHUNK, HD], F32)
+                out_tiles[chunk] = out_sb
+            out_sb = out_tiles[chunk]
+            acc_q0, acc_q1, acc_kv = acc_tiles.pop(n)
+            cross = work.tile([P, 2, ROPED_HEADS, HALF], F32)
+            for h0, acc in ((0, acc_q0), (BANK_HEADS, acc_q1)):
+                rope_products(
+                    acc[:], BANK_HEADS, cos_raw[:, t, :], sin_q[:, t, :, :],
+                    out_sb[:, h0 : h0 + BANK_HEADS, j, :], cross[:, :, h0 : h0 + BANK_HEADS, :],
+                )
+            rope_products(
+                acc_kv[:, 0 : KV_HEADS * HD], KV_HEADS, cos_k[:, t, :], sin_k[:, t, :, :],
+                out_sb[:, Q_HEADS:ROPED_HEADS, j, :], cross[:, :, Q_HEADS:ROPED_HEADS, :],
+            )
+            nc.scalar.copy(
+                out=out_sb[:, ROPED_HEADS:HEADS, j, :],
+                in_=acc_kv[:, KV_HEADS * HD :].rearrange("p (h d) -> p h d", d=HD),
+            )
+            roped = out_sb[:, 0:ROPED_HEADS, j, :].rearrange("p h (i e) -> p h i e", e=2)
+            nc.gpsimd.tensor_tensor(
+                out=roped, in0=roped, in1=cross[:].rearrange("p e h i -> p h i e"), op=ALU.add
+            )
+            if j == CHUNK - 1:
+                toks = slice(t0, t0 + CHUNK)
+                nc.sync.dma_start(out=q_view[b, :, :, toks, :], in_=out_sb[:, 0:Q_HEADS, :, :])
+                nc.sync.dma_start(
+                    out=k_view[b, :, :, toks, :], in_=out_sb[:, Q_HEADS:ROPED_HEADS, :, :]
+                )
+                nc.sync.dma_start(out=v_view[b, :, :, toks, :], in_=out_sb[:, ROPED_HEADS:HEADS, :, :])
+
+        statistics(0)
+        for step in range(TILES + 2):
+            if step % CHUNK == 0:
+                ahead = step // CHUNK + 1
+                if ahead < CHUNKS:
+                    if ahead >= 4:
+                        load_x(ahead)
+                    statistics(ahead)
+            if step < TILES:
+                normalise_and_transpose(step)
+            if 1 <= step <= TILES:
+                quantise_and_multiply(step - 1)
+            if step >= 2:
+                rope_and_store(step - 2)

@@ -91,16 +91,16 @@ def tile_block_pa_t_kernel(
         ident = const.tile([P, P], F32)
         make_identity(nc, ident[:])
 
-        sin_pairs = sin_raw[:].rearrange("p t (i e) -> p t e i", e=2)
-        sin_q = const.tile([P, TOK, 2, HALF], F32)
-        sin_k = const.tile([P, TOK, 2, HALF], F32)
+        sin_pairs = sin_raw[:].rearrange("p t (i e) -> p t i e", e=2)
+        sin_q = const.tile([P, TOK, HALF, 2], F32)
+        sin_k = const.tile([P, TOK, HALF, 2], F32)
         cos_k = const.tile([P, TOK, HD], F32)
         k_scale = HD**-0.5
         for table, scale in ((sin_q, 1.0), (sin_k, k_scale)):
             for e, sign in ((0, -1.0), (1, 1.0)):
                 nc.gpsimd.tensor_scalar(
-                    out=table[:, :, e, :],
-                    in0=sin_pairs[:, :, e, :],
+                    out=table[:, :, :, e],
+                    in0=sin_pairs[:, :, :, e],
                     scalar1=sign * scale,
                     scalar2=0.0,
                     op0=ALU.mult,
@@ -199,11 +199,11 @@ def tile_block_pa_t_kernel(
                 in1=cos_row.unsqueeze(1).to_broadcast([P, heads, HD]),
                 op=ALU.mult,
             )
-            partners = u.rearrange("p (h i e) -> p e h i", i=HALF, e=2)[:, ::-1, :, :]
+            partners = u.rearrange("p (h i e) -> p h i e", i=HALF, e=2)[:, :, :, ::-1]
             nc.vector.tensor_tensor(
                 out=cross,
                 in0=partners,
-                in1=sin_rows.unsqueeze(2).to_broadcast([P, 2, heads, HALF]),
+                in1=sin_rows.unsqueeze(1).to_broadcast([P, heads, HALF, 2]),
                 op=ALU.mult,
             )
 
@@ -216,23 +216,23 @@ def tile_block_pa_t_kernel(
                 out_tiles[chunk] = out_sb
             out_sb = out_tiles[chunk]
             acc_q0, acc_q1, acc_kv = acc_tiles.pop(n)
-            cross = work.tile([P, 2, ROPED_HEADS, HALF], F32)
+            cross = work.tile([P, ROPED_HEADS, HALF, 2], F32)
             for h0, acc in ((0, acc_q0), (BANK_HEADS, acc_q1)):
                 rope_products(
                     acc[:], BANK_HEADS, cos_raw[:, t, :], sin_q[:, t, :, :],
-                    out_sb[:, h0 : h0 + BANK_HEADS, j, :], cross[:, :, h0 : h0 + BANK_HEADS, :],
+                    out_sb[:, h0 : h0 + BANK_HEADS, j, :], cross[:, h0 : h0 + BANK_HEADS, :, :],
                 )
             rope_products(
                 acc_kv[:, 0 : KV_HEADS * HD], KV_HEADS, cos_k[:, t, :], sin_k[:, t, :, :],
-                out_sb[:, Q_HEADS:ROPED_HEADS, j, :], cross[:, :, Q_HEADS:ROPED_HEADS, :],
+                out_sb[:, Q_HEADS:ROPED_HEADS, j, :], cross[:, Q_HEADS:ROPED_HEADS, :, :],
             )
             nc.scalar.copy(
                 out=out_sb[:, ROPED_HEADS:HEADS, j, :],
                 in_=acc_kv[:, KV_HEADS * HD :].rearrange("p (h d) -> p h d", d=HD),
             )
-            roped = out_sb[:, 0:ROPED_HEADS, j, :].rearrange("p h (i e) -> p h i e", e=2)
+            roped = out_sb[:, 0:ROPED_HEADS, j, :]
             nc.gpsimd.tensor_tensor(
-                out=roped, in0=roped, in1=cross[:].rearrange("p e h i -> p h i e"), op=ALU.add
+                out=roped, in0=roped, in1=cross[:].rearrange("p h i e -> p h (i e)"), op=ALU.add
             )
             if j == CHUNK - 1:
                 toks = slice(t0, t0 + CHUNK)

@@ -28,11 +28,15 @@ PACK = 4
 K_PASS = P * PACK
 PASSES = D // K_PASS
 PAIRS = PACK // 2
+K_BLOCKS = D // P
+HALF_BLOCKS = K_BLOCKS // PASSES
 
 TOK = SEQ // P
 CHUNK = 4
 TILES = BATCH * TOK
 CHUNKS = TILES // CHUNK
+DIRECT = 2
+SQUARES_AHEAD = 8
 BANK = 512
 BANK_HEADS = BANK // HD
 
@@ -51,17 +55,26 @@ def tile_block_pa_t_kernel(
 
     with ExitStack() as ctx:
         const = ctx.enter_context(tc.tile_pool(name="const", bufs=1))
-        x_pool = ctx.enter_context(tc.tile_pool(name="x_pool", bufs=4))
+        x_pool = ctx.enter_context(tc.tile_pool(name="x_pool", bufs=CHUNKS))
         stat = ctx.enter_context(tc.tile_pool(name="stat", bufs=3))
         work = ctx.enter_context(tc.tile_pool(name="work", bufs=3))
         out_pool = ctx.enter_context(tc.tile_pool(name="out_pool", bufs=3))
-        xt_psum = ctx.enter_context(tc.psum_pool(name="xt_psum", bufs=2))
-        acc_psum = ctx.enter_context(tc.psum_pool(name="acc_psum", bufs=2))
+        flip_psum = ctx.enter_context(tc.psum_pool(name="flip_psum", bufs=1))
+        acc_psum = ctx.enter_context(tc.psum_pool(name="acc_psum", bufs=5))
 
         x_tiles = {}
+        sum_tiles = {}
+        rms_tiles = {}
         rstd_tiles = {}
+        raw_tiles = {}
+        flipped_tiles = {}
+        product_tiles = {}
+        xn_tiles = {}
+        word_tiles = {}
         grouped_tiles = {}
+        code_tiles = {}
         acc_tiles = {}
+        cross_tiles = {}
         out_tiles = {}
 
         def load_x(chunk):
@@ -81,7 +94,7 @@ def tile_block_pa_t_kernel(
         nc.sync.dma_start(out=cos_raw[:], in_=rope_cos.rearrange("(p t) d -> p t d", t=TOK))
         sin_raw = const.tile([P, TOK, HD], BF16)
         nc.sync.dma_start(out=sin_raw[:], in_=rope_sin.rearrange("(p t) d -> p t d", t=TOK))
-        for chunk in range(1, 4):
+        for chunk in range(1, CHUNKS):
             load_x(chunk)
 
         eps = const.tile([P, 1], F32)
@@ -90,6 +103,15 @@ def tile_block_pa_t_kernel(
         nc.scalar.activation(out=warm[:], in_=eps[:], func=ACT.Sqrt)
         ident = const.tile([P, P], F32)
         make_identity(nc, ident[:])
+        ident_bf = const.tile([P, P], BF16)
+        make_identity(nc, ident_bf[:])
+        gain_diag = const.tile([P, K_BLOCKS, P], BF16)
+        nc.vector.tensor_tensor(
+            out=gain_diag[:],
+            in0=gain[:].rearrange("p (kb i) -> p kb i", i=P),
+            in1=ident_bf[:].unsqueeze(1).to_broadcast([P, K_BLOCKS, P]),
+            op=ALU.mult,
+        )
 
         sin_pairs = sin_raw[:].rearrange("p t (i e) -> p t i e", e=2)
         sin_q = const.tile([P, TOK, HALF, 2], F32)
@@ -128,44 +150,104 @@ def tile_block_pa_t_kernel(
                     in_=w_grouped[:, c, n0:n1, :].rearrange("p n j -> p (n j)"),
                 )
 
-        def statistics(chunk):
-            x_sb = x_tiles[chunk]
-            sum_sq = stat.tile([P, CHUNK], F32)
-            for j in range(CHUNK):
-                squares = work.tile([P, D], BF16)
+        def square(n):
+            chunk, j = divmod(n, CHUNK)
+            if j == 0:
+                sum_sq = stat.tile([P, CHUNK], F32)
+                sum_tiles[chunk] = sum_sq
+            squares = work.tile([P, D], BF16)
+            nc.scalar.activation(
+                out=squares[:], in_=x_tiles[chunk][:, j, :], func=ACT.Square,
+                accum_out=sum_tiles[chunk][:, j : j + 1],
+            )
+            if j == CHUNK - 1:
+                rms = stat.tile([P, CHUNK], F32)
                 nc.scalar.activation(
-                    out=squares[:], in_=x_sb[:, j, :], func=ACT.Square,
-                    accum_out=sum_sq[:, j : j + 1],
+                    out=rms[:], in_=sum_tiles.pop(chunk)[:], func=ACT.Sqrt, bias=eps[:], scale=1.0 / D
                 )
-            rms = stat.tile([P, CHUNK], F32)
-            nc.scalar.activation(out=rms[:], in_=sum_sq[:], func=ACT.Sqrt, bias=eps[:], scale=1.0 / D)
+                rms_tiles[chunk] = rms
+
+        def invert(chunk):
             rstd = stat.tile([P, CHUNK], F32)
-            nc.vector.reciprocal(out=rstd[:], in_=rms[:])
+            nc.vector.reciprocal(out=rstd[:], in_=rms_tiles.pop(chunk)[:])
             rstd_tiles[chunk] = rstd
 
-        def normalise_and_transpose(n):
+        def rstd_column(n):
             chunk, j = divmod(n, CHUNK)
-            xn = work.tile([P, D], BF16)
-            nc.vector.scalar_tensor_tensor(
-                out=xn[:], in0=x_tiles[chunk][:, j, :], scalar=rstd_tiles[chunk][:, j : j + 1],
-                in1=gain[:], op0=ALU.mult, op1=ALU.mult,
-            )
-            pairs = xn[:].bitcast(F32)
-            xt = xt_psum.tile([P, PASSES, PAIRS, P], F32)
+            return rstd_tiles[chunk][:, j : j + 1]
+
+        def pair_order(row):
+            return row.rearrange("p (c i u e) -> p c u i e", c=PASSES, u=PAIRS, e=2)
+
+        def normalise_direct(n):
+            chunk, j = divmod(n, CHUNK)
+            xn = work.tile([P, PASSES, PAIRS, P, 2], BF16)
             for c in range(PASSES):
                 for u in range(PAIRS):
-                    first = c * P * PAIRS + u
-                    nc.tensor.transpose(
-                        xt[:, c, u, :], pairs[:, first : (c + 1) * P * PAIRS : PAIRS], ident[:]
+                    nc.vector.scalar_tensor_tensor(
+                        out=xn[:, c, u], in0=pair_order(x_tiles[chunk][:, j, :])[:, c, u],
+                        scalar=rstd_column(n), in1=pair_order(gain[:])[:, c, u],
+                        op0=ALU.mult, op1=ALU.mult,
                     )
-            grouped = work.tile([P, PASSES, P, PACK], BF16, align_bytes=64)
+            xn_tiles[n] = xn
+
+        def transpose_raw(n):
+            chunk, j = divmod(n, CHUNK)
+            raw = flip_psum.tile([P, K_BLOCKS, P], BF16)
+            for kb in range(K_BLOCKS):
+                nc.tensor.transpose(
+                    raw[:, kb, :], x_tiles[chunk][:, j, kb * P : (kb + 1) * P], ident_bf[:]
+                )
+            raw_tiles[n] = raw
+
+        def copy_raw(n):
+            flipped = work.tile([P, K_BLOCKS, P], BF16)
             nc.scalar.copy(
-                out=grouped[:].rearrange("p c r j -> p (c r j)").bitcast(F32),
-                in_=xt[:].rearrange("p c u r -> p c r u"),
+                out=flipped[:].rearrange("p kb r -> p (kb r)").bitcast(F32),
+                in_=raw_tiles.pop(n)[:].rearrange("p kb r -> p (kb r)").bitcast(F32),
             )
+            flipped_tiles[n] = flipped
+
+        def gain_half(n, c):
+            product = flip_psum.tile([P, BANK], F32)
+            for i in range(HALF_BLOCKS):
+                kb = c * HALF_BLOCKS + i
+                nc.tensor.matmul(
+                    product[:, i * P : (i + 1) * P], lhsT=flipped_tiles[n][:, kb, :],
+                    rhs=gain_diag[:, kb, :], start=True, stop=True,
+                )
+            product_tiles[n, c] = product
+
+        def scale_half(n, c):
+            if c == 0:
+                xn = work.tile([P, PASSES, PAIRS, P, 2], BF16)
+                xn_tiles[n] = xn
+            nc.scalar.activation(
+                out=xn_tiles[n][:, c],
+                in_=product_tiles.pop((n, c))[:].rearrange("p (i u e) -> p u i e", u=PAIRS, e=2),
+                func=ACT.Copy, scale=rstd_column(n),
+            )
+
+        def transpose_words(n):
+            pairs = xn_tiles.pop(n)[:].rearrange("p c u i e -> p (c u i e)").bitcast(F32)
+            words = flip_psum.tile([P, PASSES, PAIRS, P], F32)
+            for c in range(PASSES):
+                for u in range(PAIRS):
+                    first = (c * PAIRS + u) * P
+                    nc.tensor.transpose(words[:, c, u, :], pairs[:, first : first + P], ident[:])
+            word_tiles[n] = words
+
+        def group(n):
+            grouped = work.tile([P, PASSES, P, PACK], BF16, align_bytes=64)
+            out = grouped[:].rearrange("p c r j -> p (c r j)").bitcast(F32)
+            source = word_tiles.pop(n)[:].rearrange("p c u r -> p c r u")
+            if n % 2 == 0:
+                nc.scalar.copy(out=out, in_=source)
+            else:
+                nc.vector.tensor_copy(out=out, in_=source)
             grouped_tiles[n] = grouped
 
-        def quantise_and_multiply(n):
+        def quantise(n):
             codes = work.tile([P, PASSES, P], U32, align_bytes=64)
             scales = work.tile([P, PASSES, P], U8, align_bytes=64)
             nc.vector.quantize_mx(
@@ -173,62 +255,75 @@ def tile_block_pa_t_kernel(
                 scales=scales[:].rearrange("p c r -> p (c r)"),
                 in_=grouped_tiles.pop(n)[:].rearrange("p c r j -> p (c r j)"),
             )
-            acc_q0 = acc_psum.tile([P, BANK], F32)
-            acc_q1 = acc_psum.tile([P, BANK], F32)
-            acc_kv = acc_psum.tile([P, 2 * KV_HEADS * HD], F32)
-            n0 = 0
-            for acc in (acc_q0, acc_q1, acc_kv):
-                width = acc.shape[1]
-                for c in range(PASSES):
-                    nc.tensor.matmul_mx(
-                        out=acc[:],
-                        lhsT=codes[:, c, :].bitcast(FP8X4),
-                        lhsT_scale=scales[:, c, :],
-                        rhs=w_codes[:, c, n0 : n0 + width].bitcast(FP8X4),
-                        rhs_scale=w_scales[:, c, n0 : n0 + width],
-                        start=(c == 0),
-                        stop=(c == PASSES - 1),
-                    )
-                n0 += width
-            acc_tiles[n] = (acc_q0, acc_q1, acc_kv)
+            code_tiles[n] = (codes, scales)
 
-        def rope_products(u, heads, cos_row, sin_rows, straight, cross):
+        def multiply(n, part):
+            codes, scales = code_tiles[n]
+            n0 = part * BANK
+            width = min(BANK, N_OUT - n0)
+            acc = acc_psum.tile([P, width], F32)
+            for c in range(PASSES):
+                nc.tensor.matmul_mx(
+                    out=acc[:],
+                    lhsT=codes[:, c, :].bitcast(FP8X4),
+                    lhsT_scale=scales[:, c, :],
+                    rhs=w_codes[:, c, n0 : n0 + width].bitcast(FP8X4),
+                    rhs_scale=w_scales[:, c, n0 : n0 + width],
+                    start=(c == 0),
+                    stop=(c == PASSES - 1),
+                )
+            acc_tiles[n, part] = acc
+
+        def straight_product(u, heads, cos_row, out):
             nc.vector.tensor_tensor(
-                out=straight,
+                out=out,
                 in0=u.rearrange("p (h d) -> p h d", d=HD),
                 in1=cos_row.unsqueeze(1).to_broadcast([P, heads, HD]),
                 op=ALU.mult,
             )
-            partners = u.rearrange("p (h i e) -> p h i e", i=HALF, e=2)[:, :, :, ::-1]
+
+        def cross_product(u, heads, sin_row, out):
             nc.vector.tensor_tensor(
-                out=cross,
-                in0=partners,
-                in1=sin_rows.unsqueeze(1).to_broadcast([P, heads, HALF, 2]),
+                out=out,
+                in0=u.rearrange("p (h i e) -> p h i e", i=HALF, e=2)[:, :, :, ::-1],
+                in1=sin_row.unsqueeze(1).to_broadcast([P, heads, HALF, 2]),
                 op=ALU.mult,
             )
 
-        def rope_and_store(n):
+        def copy_v(n):
             chunk, j = divmod(n, CHUNK)
-            b, t0 = divmod(chunk * CHUNK, TOK)
-            t = t0 + j
             if j == 0:
                 out_sb = out_pool.tile([P, HEADS, CHUNK, HD], F32)
                 out_tiles[chunk] = out_sb
-            out_sb = out_tiles[chunk]
-            acc_q0, acc_q1, acc_kv = acc_tiles.pop(n)
-            cross = work.tile([P, ROPED_HEADS, HALF, 2], F32)
-            for h0, acc in ((0, acc_q0), (BANK_HEADS, acc_q1)):
-                rope_products(
-                    acc[:], BANK_HEADS, cos_raw[:, t, :], sin_q[:, t, :, :],
-                    out_sb[:, h0 : h0 + BANK_HEADS, j, :], cross[:, h0 : h0 + BANK_HEADS, :, :],
-                )
-            rope_products(
-                acc_kv[:, 0 : KV_HEADS * HD], KV_HEADS, cos_k[:, t, :], sin_k[:, t, :, :],
-                out_sb[:, Q_HEADS:ROPED_HEADS, j, :], cross[:, Q_HEADS:ROPED_HEADS, :, :],
-            )
             nc.scalar.copy(
-                out=out_sb[:, ROPED_HEADS:HEADS, j, :],
-                in_=acc_kv[:, KV_HEADS * HD :].rearrange("p (h d) -> p h d", d=HD),
+                out=out_tiles[chunk][:, ROPED_HEADS:HEADS, j, :],
+                in_=acc_tiles[n, 2][:, KV_HEADS * HD :].rearrange("p (h d) -> p h d", d=HD),
+            )
+
+        def rope_main(n):
+            chunk, j = divmod(n, CHUNK)
+            t = n % TOK
+            out_sb = out_tiles[chunk]
+            cross = work.tile([P, ROPED_HEADS, HALF, 2], F32)
+            cross_tiles[n] = cross
+            for part in range(2):
+                heads = slice(part * BANK_HEADS, (part + 1) * BANK_HEADS)
+                acc = acc_tiles.pop((n, part))
+                straight_product(acc[:], BANK_HEADS, cos_raw[:, t, :], out_sb[:, heads, j, :])
+                cross_product(acc[:], BANK_HEADS, sin_q[:, t, :, :], cross[:, heads, :, :])
+            straight_product(
+                acc_tiles[n, 2][:, 0 : KV_HEADS * HD], KV_HEADS, cos_k[:, t, :],
+                out_sb[:, Q_HEADS:ROPED_HEADS, j, :],
+            )
+
+        def rope_rest(n):
+            chunk, j = divmod(n, CHUNK)
+            b, t0 = divmod(chunk * CHUNK, TOK)
+            out_sb = out_tiles[chunk]
+            cross = cross_tiles.pop(n)
+            cross_product(
+                acc_tiles.pop((n, 2))[:, 0 : KV_HEADS * HD], KV_HEADS, sin_k[:, t0 + j, :, :],
+                cross[:, Q_HEADS:ROPED_HEADS, :, :],
             )
             roped = out_sb[:, 0:ROPED_HEADS, j, :]
             nc.gpsimd.tensor_tensor(
@@ -242,17 +337,45 @@ def tile_block_pa_t_kernel(
                 )
                 nc.sync.dma_start(out=v_view[b, :, :, toks, :], in_=out_sb[:, ROPED_HEADS:HEADS, :, :])
 
-        statistics(0)
-        for step in range(TILES + 2):
-            if step % CHUNK == 0:
-                ahead = step // CHUNK + 1
-                if ahead < CHUNKS:
-                    if ahead >= 4:
-                        load_x(ahead)
-                    statistics(ahead)
-            if step < TILES:
-                normalise_and_transpose(step)
-            if 1 <= step <= TILES:
-                quantise_and_multiply(step - 1)
-            if step >= 2:
-                rope_and_store(step - 2)
+        with tc.manual_schedule():
+            for n in range(CHUNK):
+                square(n)
+            for step in range(-4, TILES + 1):
+                def has(n, first=0):
+                    return first <= n < TILES
+
+                if has(step + 1):
+                    quantise(step + 1)
+                if has(step - 1):
+                    rope_rest(step - 1)
+                if step % CHUNK == 0 and has(step + CHUNK):
+                    invert(step // CHUNK + 1)
+                if 0 <= step + 3 < DIRECT:
+                    normalise_direct(step + 3)
+                if has(step + 2):
+                    transpose_words(step + 2)
+                if has(step + 5, DIRECT):
+                    transpose_raw(step + 5)
+                if has(step + 3, DIRECT):
+                    scale_half(step + 3, 1)
+                if has(step):
+                    copy_v(step)
+                if has(step + 2):
+                    group(step + 2)
+                if has(step + 5, DIRECT):
+                    copy_raw(step + 5)
+                if has(step + 1):
+                    multiply(step + 1, 0)
+                if has(step + 4, DIRECT):
+                    gain_half(step + 4, 0)
+                    scale_half(step + 4, 0)
+                if has(step + 1):
+                    multiply(step + 1, 1)
+                if has(step + 4, DIRECT):
+                    gain_half(step + 4, 1)
+                if has(step + 1):
+                    multiply(step + 1, 2)
+                if has(step):
+                    rope_main(step)
+                if has(step + SQUARES_AHEAD):
+                    square(step + SQUARES_AHEAD)

@@ -29,16 +29,15 @@ K_PASS = P * PACK
 PASSES = D // K_PASS
 PAIRS = PACK // 2
 K_BLOCKS = D // P
-HALF_BLOCKS = K_BLOCKS // PASSES
+PASS_BLOCKS = K_BLOCKS // PASSES
 
 TOK = SEQ // P
-CHUNK = 4
 TILES = BATCH * TOK
-CHUNKS = TILES // CHUNK
-DIRECT = 2
-SQUARES_AHEAD = 8
+GROUP = 2
+CHUNK = 4
 BANK = 512
 BANK_HEADS = BANK // HD
+PARTS = ((0, 512), (512, 1024), (1024, N_OUT))
 
 FLOPS = 2 * BATCH * SEQ * D * N_OUT
 
@@ -55,7 +54,7 @@ def tile_block_pa_t_kernel(
 
     with ExitStack() as ctx:
         const = ctx.enter_context(tc.tile_pool(name="const", bufs=1))
-        x_pool = ctx.enter_context(tc.tile_pool(name="x_pool", bufs=CHUNKS))
+        x_pool = ctx.enter_context(tc.tile_pool(name="x_pool", bufs=14))
         stat = ctx.enter_context(tc.tile_pool(name="stat", bufs=3))
         work = ctx.enter_context(tc.tile_pool(name="work", bufs=3))
         out_pool = ctx.enter_context(tc.tile_pool(name="out_pool", bufs=3))
@@ -77,155 +76,156 @@ def tile_block_pa_t_kernel(
         cross_tiles = {}
         out_tiles = {}
 
-        def load_x(chunk):
-            b, t0 = divmod(chunk * CHUNK, TOK)
-            x_sb = x_pool.tile([P, CHUNK, D], BF16)
-            nc.sync.dma_start(out=x_sb[:], in_=x_view[b, :, t0 : t0 + CHUNK, :])
-            x_tiles[chunk] = x_sb
+        gain_rows = const.tile([P, P], BF16)
+        nc.vector.memset(gain_rows[:], 0.0)
+        nc.scalar.dma_start(out=gain_rows[0:K_BLOCKS, :], in_=norm1_w.rearrange("(kb i) -> kb i", i=P))
 
-        load_x(0)
-        gain = const.tile([P, D], BF16)
-        nc.scalar.dma_start(out=gain[:], in_=norm1_w.partition_broadcast(P))
+        def load_x(group):
+            b, t0 = divmod(group * GROUP, TOK)
+            x_sb = x_pool.tile([P, GROUP, D], BF16)
+            size = 1 if group == 0 else GROUP
+            for j in range(0, GROUP, size):
+                nc.sync.dma_start(
+                    out=x_sb[:, j : j + size, :], in_=x_view[b, :, t0 + j : t0 + j + size, :]
+                )
+            x_tiles[group] = x_sb
+
         w_raw = const.tile([P, PASSES, PACK, N_OUT], BF16)
         w_rows = wqkv.rearrange("(c p j) n -> p c j n", p=P, j=PACK)
-        for c in range(PASSES):
-            nc.sync.dma_start(out=w_raw[:, c, :, :], in_=w_rows[:, c, :, :])
-        cos_raw = const.tile([P, TOK, HD], BF16)
-        nc.sync.dma_start(out=cos_raw[:], in_=rope_cos.rearrange("(p t) d -> p t d", t=TOK))
+
+        def load_w(part, c):
+            n0, n1 = PARTS[part]
+            nc.sync.dma_start(out=w_raw[:, c, :, n0:n1], in_=w_rows[:, c, :, n0:n1])
+
+        load_w(0, 0)
+        load_x(0)
+        load_w(0, 1)
+        load_x(1)
+        load_w(1, 0)
+        load_w(1, 1)
+        load_x(2)
+        load_w(2, 0)
+        load_w(2, 1)
+        cos_q = const.tile([P, TOK, HD], BF16)
+        nc.sync.dma_start(out=cos_q[:], in_=rope_cos.rearrange("(p t) d -> p t d", t=TOK))
         sin_raw = const.tile([P, TOK, HD], BF16)
         nc.sync.dma_start(out=sin_raw[:], in_=rope_sin.rearrange("(p t) d -> p t d", t=TOK))
-        for chunk in range(1, CHUNKS):
-            load_x(chunk)
+        for group in range(3, TILES // GROUP):
+            load_x(group)
 
         eps = const.tile([P, 1], F32)
         nc.vector.memset(eps[:], EPS)
         warm = const.tile([P, 1], F32)
         nc.scalar.activation(out=warm[:], in_=eps[:], func=ACT.Sqrt)
-        ident = const.tile([P, P], F32)
-        make_identity(nc, ident[:])
         ident_bf = const.tile([P, P], BF16)
         make_identity(nc, ident_bf[:])
-        gain_diag = const.tile([P, K_BLOCKS, P], BF16)
-        nc.vector.tensor_tensor(
-            out=gain_diag[:],
-            in0=gain[:].rearrange("p (kb i) -> p kb i", i=P),
-            in1=ident_bf[:].unsqueeze(1).to_broadcast([P, K_BLOCKS, P]),
-            op=ALU.mult,
-        )
-
-        sin_pairs = sin_raw[:].rearrange("p t (i e) -> p t i e", e=2)
-        sin_q = const.tile([P, TOK, HALF, 2], F32)
-        sin_k = const.tile([P, TOK, HALF, 2], F32)
-        cos_k = const.tile([P, TOK, HD], F32)
-        k_scale = HD**-0.5
-        for table, scale in ((sin_q, 1.0), (sin_k, k_scale)):
-            for e, sign in ((0, -1.0), (1, 1.0)):
-                nc.gpsimd.tensor_scalar(
-                    out=table[:, :, :, e],
-                    in0=sin_pairs[:, :, :, e],
-                    scalar1=sign * scale,
-                    scalar2=0.0,
-                    op0=ALU.mult,
-                    op1=ALU.add,
-                )
-        nc.gpsimd.tensor_scalar(
-            out=cos_k[:], in0=cos_raw[:], scalar1=k_scale, scalar2=0.0, op0=ALU.mult, op1=ALU.add
-        )
+        ident = const.tile([P, P], F32)
+        make_identity(nc, ident[:])
+        signs = const.tile([P, HALF, 2], BF16)
+        nc.vector.memset(signs[:, :, 0], -1.0)
+        nc.vector.memset(signs[:, :, 1], 1.0)
 
         w_grouped = const.tile([P, PASSES, N_OUT, PACK], BF16, align_bytes=64)
         w_codes = const.tile([P, PASSES, N_OUT], U32, align_bytes=64)
         w_scales = const.tile([P, PASSES, N_OUT], U8, align_bytes=64)
-        for c in range(PASSES):
-            src = w_raw[:, c, :, :].rearrange("p j (m i) -> p m j i", i=4)
-            dst = w_grouped[:, c, :, :].rearrange("p (m i) j -> p m j i", i=4)
-            if c == 0:
-                nc.vector.tensor_copy(out=dst, in_=src)
-            else:
-                nc.scalar.copy(out=dst, in_=src)
-        for c in range(PASSES):
-            for n0, n1 in ((0, 1024), (1024, N_OUT)):
-                nc.vector.quantize_mx(
-                    out=w_codes[:, c, n0:n1].bitcast(FP8X4),
-                    scales=w_scales[:, c, n0:n1],
-                    in_=w_grouped[:, c, n0:n1, :].rearrange("p n j -> p (n j)"),
+        gain_diag = const.tile([P, K_BLOCKS, P], BF16)
+        sin_q = const.tile([P, TOK, HD], BF16)
+        sin_k = const.tile([P, TOK, HD], BF16)
+        cos_k = const.tile([P, TOK, HD], BF16)
+
+        def make_gain_diag():
+            raw = flip_psum.tile([P, K_BLOCKS, P], BF16)
+            nc.tensor.transpose(raw[:, 0, :], gain_rows[:], ident_bf[:])
+            gain_columns = const.tile([P, K_BLOCKS], F32)
+            nc.vector.tensor_copy(out=gain_columns[:], in_=raw[:, 0, 0:K_BLOCKS])
+            for kb in range(K_BLOCKS):
+                nc.vector.tensor_scalar(
+                    out=gain_diag[:, kb, :], in0=ident_bf[:], scalar1=gain_columns[:, kb : kb + 1],
+                    scalar2=None, op0=ALU.mult,
                 )
+
+        def make_rope_tables():
+            nc.vector.tensor_tensor(
+                out=sin_q[:], in0=sin_raw[:],
+                in1=signs[:].rearrange("p i e -> p (i e)").unsqueeze(1).to_broadcast([P, TOK, HD]),
+                op=ALU.mult,
+            )
+            for k_table, q_table in ((sin_k, sin_q), (cos_k, cos_q)):
+                nc.vector.tensor_scalar(
+                    out=k_table[:], in0=q_table[:], scalar1=HD**-0.5, scalar2=None, op0=ALU.mult
+                )
+
+        def group_w(part, c):
+            n0, n1 = PARTS[part]
+            nc.vector.tensor_copy(
+                out=w_grouped[:, c, n0:n1, :].rearrange("p (m i) j -> p m j i", i=4),
+                in_=w_raw[:, c, :, n0:n1].rearrange("p j (m i) -> p m j i", i=4),
+            )
+
+        def quantise_w(part, c):
+            n0, n1 = PARTS[part]
+            nc.vector.quantize_mx(
+                out=w_codes[:, c, n0:n1].bitcast(FP8X4),
+                scales=w_scales[:, c, n0:n1],
+                in_=w_grouped[:, c, n0:n1, :].rearrange("p n j -> p (n j)"),
+            )
+
+        def x_row(n):
+            return x_tiles[n // GROUP][:, n % GROUP, :]
 
         def square(n):
-            chunk, j = divmod(n, CHUNK)
+            group, j = divmod(n, GROUP)
             if j == 0:
-                sum_sq = stat.tile([P, CHUNK], F32)
-                sum_tiles[chunk] = sum_sq
+                sum_sq = stat.tile([P, GROUP], F32)
+                sum_tiles[group] = sum_sq
             squares = work.tile([P, D], BF16)
             nc.scalar.activation(
-                out=squares[:], in_=x_tiles[chunk][:, j, :], func=ACT.Square,
-                accum_out=sum_tiles[chunk][:, j : j + 1],
+                out=squares[:], in_=x_row(n), func=ACT.Square, accum_out=sum_tiles[group][:, j : j + 1]
             )
-            if j == CHUNK - 1:
-                rms = stat.tile([P, CHUNK], F32)
+            if j == GROUP - 1:
+                rms = stat.tile([P, GROUP], F32)
                 nc.scalar.activation(
-                    out=rms[:], in_=sum_tiles.pop(chunk)[:], func=ACT.Sqrt, bias=eps[:], scale=1.0 / D
+                    out=rms[:], in_=sum_tiles.pop(group)[:], func=ACT.Sqrt, bias=eps[:], scale=1.0 / D
                 )
-                rms_tiles[chunk] = rms
+                rms_tiles[group] = rms
 
-        def invert(chunk):
-            rstd = stat.tile([P, CHUNK], F32)
-            nc.vector.reciprocal(out=rstd[:], in_=rms_tiles.pop(chunk)[:])
-            rstd_tiles[chunk] = rstd
-
-        def rstd_column(n):
-            chunk, j = divmod(n, CHUNK)
-            return rstd_tiles[chunk][:, j : j + 1]
-
-        def pair_order(row):
-            return row.rearrange("p (c i u e) -> p c u i e", c=PASSES, u=PAIRS, e=2)
-
-        def normalise_direct(n):
-            chunk, j = divmod(n, CHUNK)
-            xn = work.tile([P, PASSES, PAIRS, P, 2], BF16)
-            for c in range(PASSES):
-                for u in range(PAIRS):
-                    nc.vector.scalar_tensor_tensor(
-                        out=xn[:, c, u], in0=pair_order(x_tiles[chunk][:, j, :])[:, c, u],
-                        scalar=rstd_column(n), in1=pair_order(gain[:])[:, c, u],
-                        op0=ALU.mult, op1=ALU.mult,
-                    )
-            xn_tiles[n] = xn
+        def invert(group):
+            rstd = stat.tile([P, GROUP], F32)
+            nc.vector.reciprocal(out=rstd[:], in_=rms_tiles.pop(group)[:])
+            rstd_tiles[group] = rstd
 
         def transpose_raw(n):
-            chunk, j = divmod(n, CHUNK)
             raw = flip_psum.tile([P, K_BLOCKS, P], BF16)
             for kb in range(K_BLOCKS):
-                nc.tensor.transpose(
-                    raw[:, kb, :], x_tiles[chunk][:, j, kb * P : (kb + 1) * P], ident_bf[:]
-                )
+                nc.tensor.transpose(raw[:, kb, :], x_row(n)[:, kb * P : (kb + 1) * P], ident_bf[:])
             raw_tiles[n] = raw
 
         def copy_raw(n):
             flipped = work.tile([P, K_BLOCKS, P], BF16)
-            nc.scalar.copy(
-                out=flipped[:].rearrange("p kb r -> p (kb r)").bitcast(F32),
-                in_=raw_tiles.pop(n)[:].rearrange("p kb r -> p (kb r)").bitcast(F32),
-            )
+            out = flipped[:].rearrange("p kb r -> p (kb r)").bitcast(F32)
+            source = raw_tiles.pop(n)[:].rearrange("p kb r -> p (kb r)").bitcast(F32)
+            nc.scalar.copy(out=out, in_=source)
             flipped_tiles[n] = flipped
 
-        def gain_half(n, c):
+        def multiply_gain(n, c):
             product = flip_psum.tile([P, BANK], F32)
-            for i in range(HALF_BLOCKS):
-                kb = c * HALF_BLOCKS + i
+            for i in range(PASS_BLOCKS):
+                kb = c * PASS_BLOCKS + i
                 nc.tensor.matmul(
                     product[:, i * P : (i + 1) * P], lhsT=flipped_tiles[n][:, kb, :],
                     rhs=gain_diag[:, kb, :], start=True, stop=True,
                 )
             product_tiles[n, c] = product
 
-        def scale_half(n, c):
+        def scale(n, c):
+            group, j = divmod(n, GROUP)
             if c == 0:
                 xn = work.tile([P, PASSES, PAIRS, P, 2], BF16)
                 xn_tiles[n] = xn
             nc.scalar.activation(
                 out=xn_tiles[n][:, c],
                 in_=product_tiles.pop((n, c))[:].rearrange("p (i u e) -> p u i e", u=PAIRS, e=2),
-                func=ACT.Copy, scale=rstd_column(n),
+                func=ACT.Copy, scale=rstd_tiles[group][:, j : j + 1],
             )
 
         def transpose_words(n):
@@ -237,58 +237,44 @@ def tile_block_pa_t_kernel(
                     nc.tensor.transpose(words[:, c, u, :], pairs[:, first : first + P], ident[:])
             word_tiles[n] = words
 
-        def group(n):
-            grouped = work.tile([P, PASSES, P, PACK], BF16, align_bytes=64)
-            out = grouped[:].rearrange("p c r j -> p (c r j)").bitcast(F32)
+        def group_x(n):
+            group, j = divmod(n, GROUP)
+            if j == 0:
+                grouped = work.tile([P, GROUP, PASSES, P, PACK], BF16, align_bytes=64)
+                grouped_tiles[group] = grouped
+            out = grouped_tiles[group][:, j].rearrange("p c r j -> p (c r j)").bitcast(F32)
             source = word_tiles.pop(n)[:].rearrange("p c u r -> p c r u")
-            if n % 2 == 0:
-                nc.scalar.copy(out=out, in_=source)
-            else:
+            if n % 4 != 0:
                 nc.vector.tensor_copy(out=out, in_=source)
-            grouped_tiles[n] = grouped
+            else:
+                nc.scalar.copy(out=out, in_=source)
 
-        def quantise(n):
-            codes = work.tile([P, PASSES, P], U32, align_bytes=64)
-            scales = work.tile([P, PASSES, P], U8, align_bytes=64)
+        def quantise_x(group):
+            codes = work.tile([P, GROUP, PASSES, P], U32, align_bytes=64)
+            scales = work.tile([P, GROUP, PASSES, P], U8, align_bytes=64)
             nc.vector.quantize_mx(
-                out=codes[:].rearrange("p c r -> p (c r)").bitcast(FP8X4),
-                scales=scales[:].rearrange("p c r -> p (c r)"),
-                in_=grouped_tiles.pop(n)[:].rearrange("p c r j -> p (c r j)"),
+                out=codes[:].rearrange("p g c r -> p (g c r)").bitcast(FP8X4),
+                scales=scales[:].rearrange("p g c r -> p (g c r)"),
+                in_=grouped_tiles.pop(group)[:].rearrange("p g c r j -> p (g c r j)"),
             )
-            code_tiles[n] = (codes, scales)
+            code_tiles[group] = (codes, scales)
 
         def multiply(n, part):
-            codes, scales = code_tiles[n]
-            n0 = part * BANK
-            width = min(BANK, N_OUT - n0)
-            acc = acc_psum.tile([P, width], F32)
+            group, j = divmod(n, GROUP)
+            codes, scales = code_tiles[group]
+            n0, n1 = PARTS[part]
+            acc = acc_psum.tile([P, n1 - n0], F32)
             for c in range(PASSES):
                 nc.tensor.matmul_mx(
                     out=acc[:],
-                    lhsT=codes[:, c, :].bitcast(FP8X4),
-                    lhsT_scale=scales[:, c, :],
-                    rhs=w_codes[:, c, n0 : n0 + width].bitcast(FP8X4),
-                    rhs_scale=w_scales[:, c, n0 : n0 + width],
+                    lhsT=codes[:, j, c, :].bitcast(FP8X4),
+                    lhsT_scale=scales[:, j, c, :],
+                    rhs=w_codes[:, c, n0:n1].bitcast(FP8X4),
+                    rhs_scale=w_scales[:, c, n0:n1],
                     start=(c == 0),
                     stop=(c == PASSES - 1),
                 )
             acc_tiles[n, part] = acc
-
-        def straight_product(u, heads, cos_row, out):
-            nc.vector.tensor_tensor(
-                out=out,
-                in0=u.rearrange("p (h d) -> p h d", d=HD),
-                in1=cos_row.unsqueeze(1).to_broadcast([P, heads, HD]),
-                op=ALU.mult,
-            )
-
-        def cross_product(u, heads, sin_row, out):
-            nc.vector.tensor_tensor(
-                out=out,
-                in0=u.rearrange("p (h i e) -> p h i e", i=HALF, e=2)[:, :, :, ::-1],
-                in1=sin_row.unsqueeze(1).to_broadcast([P, heads, HALF, 2]),
-                op=ALU.mult,
-            )
 
         def copy_v(n):
             chunk, j = divmod(n, CHUNK)
@@ -300,82 +286,138 @@ def tile_block_pa_t_kernel(
                 in_=acc_tiles[n, 2][:, KV_HEADS * HD :].rearrange("p (h d) -> p h d", d=HD),
             )
 
-        def rope_main(n):
+        def straight_product(u, heads, cos_row, out):
+            nc.vector.tensor_tensor(
+                out=out,
+                in0=u.rearrange("p (h d) -> p h d", d=HD),
+                in1=cos_row.unsqueeze(1).to_broadcast([P, heads, HD]),
+                op=ALU.mult,
+            )
+
+        def cross_product(u, heads, sin_row, out):
+            nc.vector.tensor_tensor(
+                out=out.rearrange("p h (i e) -> p h i e", e=2),
+                in0=u.rearrange("p (h i e) -> p h i e", i=HALF, e=2)[:, :, :, ::-1],
+                in1=sin_row.rearrange("p (i e) -> p i e", e=2)
+                .unsqueeze(1)
+                .to_broadcast([P, heads, HALF, 2]),
+                op=ALU.mult,
+            )
+
+        def rope_products(n, part):
             chunk, j = divmod(n, CHUNK)
             t = n % TOK
             out_sb = out_tiles[chunk]
-            cross = work.tile([P, ROPED_HEADS, HALF, 2], F32)
-            cross_tiles[n] = cross
-            for part in range(2):
+            if part == 2:
+                straight_product(
+                    acc_tiles[n, 2][:, 0 : KV_HEADS * HD], KV_HEADS, cos_k[:, t, :],
+                    out_sb[:, Q_HEADS:ROPED_HEADS, j, :],
+                )
+            else:
+                if part == 0:
+                    cross = work.tile([P, ROPED_HEADS, HD], F32)
+                    cross_tiles[n] = cross
                 heads = slice(part * BANK_HEADS, (part + 1) * BANK_HEADS)
                 acc = acc_tiles.pop((n, part))
-                straight_product(acc[:], BANK_HEADS, cos_raw[:, t, :], out_sb[:, heads, j, :])
-                cross_product(acc[:], BANK_HEADS, sin_q[:, t, :, :], cross[:, heads, :, :])
-            straight_product(
-                acc_tiles[n, 2][:, 0 : KV_HEADS * HD], KV_HEADS, cos_k[:, t, :],
-                out_sb[:, Q_HEADS:ROPED_HEADS, j, :],
+                straight_product(acc[:], BANK_HEADS, cos_q[:, t, :], out_sb[:, heads, j, :])
+                cross_product(acc[:], BANK_HEADS, sin_q[:, t, :], cross_tiles[n][:, heads, :])
+
+        def rope_partner_k(n):
+            cross_product(
+                acc_tiles.pop((n, 2))[:, 0 : KV_HEADS * HD], KV_HEADS, sin_k[:, n % TOK, :],
+                cross_tiles[n][:, Q_HEADS:ROPED_HEADS, :],
             )
 
-        def rope_rest(n):
+        def add_partners(engine, n, h0, h1):
             chunk, j = divmod(n, CHUNK)
-            b, t0 = divmod(chunk * CHUNK, TOK)
-            out_sb = out_tiles[chunk]
-            cross = cross_tiles.pop(n)
-            cross_product(
-                acc_tiles.pop((n, 2))[:, 0 : KV_HEADS * HD], KV_HEADS, sin_k[:, t0 + j, :, :],
-                cross[:, Q_HEADS:ROPED_HEADS, :, :],
-            )
-            roped = out_sb[:, 0:ROPED_HEADS, j, :]
-            nc.gpsimd.tensor_tensor(
-                out=roped, in0=roped, in1=cross[:].rearrange("p h i e -> p h (i e)"), op=ALU.add
-            )
-            if j == CHUNK - 1:
-                toks = slice(t0, t0 + CHUNK)
-                nc.sync.dma_start(out=q_view[b, :, :, toks, :], in_=out_sb[:, 0:Q_HEADS, :, :])
-                nc.sync.dma_start(
-                    out=k_view[b, :, :, toks, :], in_=out_sb[:, Q_HEADS:ROPED_HEADS, :, :]
-                )
-                nc.sync.dma_start(out=v_view[b, :, :, toks, :], in_=out_sb[:, ROPED_HEADS:HEADS, :, :])
+            roped = out_tiles[chunk][:, h0:h1, j, :]
+            engine.tensor_tensor(out=roped, in0=roped, in1=cross_tiles[n][:, h0:h1, :], op=ALU.add)
+
+        def store(n0, n1, h0, h1):
+            chunk, j0 = divmod(n0, CHUNK)
+            b, t0 = divmod(n0, TOK)
+            toks = slice(t0, t0 + n1 - n0)
+            for view, first, last in (
+                (q_view, 0, Q_HEADS), (k_view, Q_HEADS, ROPED_HEADS), (v_view, ROPED_HEADS, HEADS)
+            ):
+                a, z = max(h0, first), min(h1, last)
+                if a < z:
+                    nc.sync.dma_start(
+                        out=view[b, :, a - first : z - first, toks, :],
+                        in_=out_tiles[chunk][:, a:z, j0 : j0 + n1 - n0, :],
+                    )
+
+        def finish(n):
+            rope_partner_k(n)
+            if n < TILES - 1:
+                add_partners(nc.gpsimd, n, 0, ROPED_HEADS)
+                if n < TILES - CHUNK:
+                    if n % CHUNK == CHUNK - 1:
+                        store(n - CHUNK + 1, n + 1, 0, HEADS)
+                elif n % GROUP == 0:
+                    store(n, n + 1, 0, HEADS)
+                else:
+                    store(n, n + 1, 0, HEADS)
+            else:
+                store(n, n + 1, ROPED_HEADS, HEADS)
+                for h0, h1 in ((0, BANK_HEADS), (BANK_HEADS, Q_HEADS), (Q_HEADS, ROPED_HEADS)):
+                    add_partners(nc.vector, n, h0, h1)
+                    store(n, n + 1, h0, h1)
+
+        def exists(n):
+            return 0 <= n < TILES
+
+        w_work = {
+            -7: ((group_w, 0, 0), (group_w, 0, 1)),
+            -5: ((quantise_w, 0, 0), (quantise_w, 0, 1)),
+            -4: ((group_w, 1, 0), (group_w, 1, 1)),
+            -3: ((quantise_w, 1, 0), (quantise_w, 1, 1), (group_w, 2, 0)),
+            -2: ((group_w, 2, 1),),
+            -1: ((quantise_w, 2, 0), (quantise_w, 2, 1)),
+        }
 
         with tc.manual_schedule():
-            for n in range(CHUNK):
-                square(n)
-            for step in range(-4, TILES + 1):
-                def has(n, first=0):
-                    return first <= n < TILES
-
-                if has(step + 1):
-                    quantise(step + 1)
-                if has(step - 1):
-                    rope_rest(step - 1)
-                if step % CHUNK == 0 and has(step + CHUNK):
-                    invert(step // CHUNK + 1)
-                if 0 <= step + 3 < DIRECT:
-                    normalise_direct(step + 3)
-                if has(step + 2):
-                    transpose_words(step + 2)
-                if has(step + 5, DIRECT):
+            make_gain_diag()
+            for step in range(-7, TILES):
+                odd = step % GROUP == 1
+                if odd and exists(step + 1):
+                    quantise_x((step + 1) // GROUP)
+                if odd and exists(step - 1):
+                    finish(step - 1)
+                if exists(step + 5):
                     transpose_raw(step + 5)
-                if has(step + 3, DIRECT):
-                    scale_half(step + 3, 1)
-                if has(step):
+                if exists(step + 3):
+                    transpose_words(step + 3)
+                if exists(step):
                     copy_v(step)
-                if has(step + 2):
-                    group(step + 2)
-                if has(step + 5, DIRECT):
+                if exists(step + 4):
+                    scale(step + 4, 0)
+                if exists(step + 5):
                     copy_raw(step + 5)
-                if has(step + 1):
+                if exists(step):
+                    rope_products(step, 0)
+                if exists(step + 3):
+                    group_x(step + 3)
+                if exists(step + 1):
                     multiply(step + 1, 0)
-                if has(step + 4, DIRECT):
-                    gain_half(step + 4, 0)
-                    scale_half(step + 4, 0)
-                if has(step + 1):
+                if exists(step + 4):
+                    multiply_gain(step + 4, 1)
+                    scale(step + 4, 1)
+                if exists(step + 7):
+                    square(step + 7)
+                for job, part, c in w_work.get(step, ()):
+                    job(part, c)
+                if odd and exists(step + 5):
+                    invert((step + 5) // GROUP)
+                if step == -1:
+                    make_rope_tables()
+                if exists(step):
+                    rope_products(step, 1)
+                    rope_products(step, 2)
+                if exists(step + 1):
                     multiply(step + 1, 1)
-                if has(step + 4, DIRECT):
-                    gain_half(step + 4, 1)
-                if has(step + 1):
                     multiply(step + 1, 2)
-                if has(step):
-                    rope_main(step)
-                if has(step + SQUARES_AHEAD):
-                    square(step + SQUARES_AHEAD)
+                if exists(step + 5):
+                    multiply_gain(step + 5, 0)
+                if odd and exists(step):
+                    finish(step)

@@ -57,13 +57,14 @@ def tile_block_pa_t_kernel(
         x_pool = ctx.enter_context(tc.tile_pool(name="x_pool", bufs=14))
         stat = ctx.enter_context(tc.tile_pool(name="stat", bufs=3))
         work = ctx.enter_context(tc.tile_pool(name="work", bufs=3))
+        cross_pool = ctx.enter_context(tc.tile_pool(name="cross_pool", bufs=2))
         out_pool = ctx.enter_context(tc.tile_pool(name="out_pool", bufs=3))
         flip_psum = ctx.enter_context(tc.psum_pool(name="flip_psum", bufs=1))
-        acc_psum = ctx.enter_context(tc.psum_pool(name="acc_psum", bufs=5))
+        q_psum = ctx.enter_context(tc.psum_pool(name="q_psum", bufs=4))
+        kv_psum = ctx.enter_context(tc.psum_pool(name="kv_psum", bufs=1))
 
         x_tiles = {}
         sum_tiles = {}
-        rms_tiles = {}
         rstd_tiles = {}
         raw_tiles = {}
         flipped_tiles = {}
@@ -78,7 +79,7 @@ def tile_block_pa_t_kernel(
 
         gain_rows = const.tile([P, P], BF16)
         nc.vector.memset(gain_rows[:], 0.0)
-        nc.scalar.dma_start(out=gain_rows[0:K_BLOCKS, :], in_=norm1_w.rearrange("(kb i) -> kb i", i=P))
+        nc.sync.dma_start(out=gain_rows[0:K_BLOCKS, :], in_=norm1_w.rearrange("(kb i) -> kb i", i=P))
 
         def load_x(group):
             b, t0 = divmod(group * GROUP, TOK)
@@ -88,6 +89,8 @@ def tile_block_pa_t_kernel(
                 nc.sync.dma_start(
                     out=x_sb[:, j : j + size, :], in_=x_view[b, :, t0 + j : t0 + j + size, :]
                 )
+                if group == 0:
+                    load_w(0, j)
             x_tiles[group] = x_sb
 
         w_raw = const.tile([P, PASSES, PACK, N_OUT], BF16)
@@ -97,26 +100,24 @@ def tile_block_pa_t_kernel(
             n0, n1 = PARTS[part]
             nc.sync.dma_start(out=w_raw[:, c, :, n0:n1], in_=w_rows[:, c, :, n0:n1])
 
-        load_w(0, 0)
         load_x(0)
-        load_w(0, 1)
         load_x(1)
         load_w(1, 0)
         load_w(1, 1)
         load_x(2)
-        load_w(2, 0)
-        load_w(2, 1)
         cos_q = const.tile([P, TOK, HD], BF16)
         nc.sync.dma_start(out=cos_q[:], in_=rope_cos.rearrange("(p t) d -> p t d", t=TOK))
         sin_raw = const.tile([P, TOK, HD], BF16)
         nc.sync.dma_start(out=sin_raw[:], in_=rope_sin.rearrange("(p t) d -> p t d", t=TOK))
+        load_w(2, 0)
+        load_w(2, 1)
         for group in range(3, TILES // GROUP):
             load_x(group)
 
         eps = const.tile([P, 1], F32)
         nc.vector.memset(eps[:], EPS)
         warm = const.tile([P, 1], F32)
-        nc.scalar.activation(out=warm[:], in_=eps[:], func=ACT.Sqrt)
+        nc.scalar.activation(out=warm[:], in_=eps[:], func=ACT.Abs_reciprocal_sqrt)
         ident_bf = const.tile([P, P], BF16)
         make_identity(nc, ident_bf[:])
         ident = const.tile([P, P], F32)
@@ -183,16 +184,12 @@ def tile_block_pa_t_kernel(
                 out=squares[:], in_=x_row(n), func=ACT.Square, accum_out=sum_tiles[group][:, j : j + 1]
             )
             if j == GROUP - 1:
-                rms = stat.tile([P, GROUP], F32)
+                rstd = stat.tile([P, GROUP], F32)
                 nc.scalar.activation(
-                    out=rms[:], in_=sum_tiles.pop(group)[:], func=ACT.Sqrt, bias=eps[:], scale=1.0 / D
+                    out=rstd[:], in_=sum_tiles.pop(group)[:], func=ACT.Abs_reciprocal_sqrt,
+                    bias=eps[:], scale=1.0 / D,
                 )
-                rms_tiles[group] = rms
-
-        def invert(group):
-            rstd = stat.tile([P, GROUP], F32)
-            nc.vector.reciprocal(out=rstd[:], in_=rms_tiles.pop(group)[:])
-            rstd_tiles[group] = rstd
+                rstd_tiles[group] = rstd
 
         def transpose_raw(n):
             raw = flip_psum.tile([P, K_BLOCKS, P], BF16)
@@ -263,10 +260,18 @@ def tile_block_pa_t_kernel(
             group, j = divmod(n, GROUP)
             codes, scales = code_tiles[group]
             n0, n1 = PARTS[part]
-            acc = acc_psum.tile([P, n1 - n0], F32)
+            if part < 2:
+                q_acc = q_psum.tile([P, BANK], F32)
+                acc_tiles[n, part] = q_acc
+                acc = q_acc[:]
+            else:
+                if j == 0:
+                    kv_acc = kv_psum.tile([P, GROUP, n1 - n0], F32)
+                    acc_tiles[group] = kv_acc
+                acc = acc_tiles[group][:, j, :]
             for c in range(PASSES):
                 nc.tensor.matmul_mx(
-                    out=acc[:],
+                    out=acc,
                     lhsT=codes[:, j, c, :].bitcast(FP8X4),
                     lhsT_scale=scales[:, j, c, :],
                     rhs=w_codes[:, c, n0:n1].bitcast(FP8X4),
@@ -274,64 +279,71 @@ def tile_block_pa_t_kernel(
                     start=(c == 0),
                     stop=(c == PASSES - 1),
                 )
-            acc_tiles[n, part] = acc
 
-        def copy_v(n):
+        def copy_v(group):
+            chunk, j = divmod(group * GROUP, CHUNK)
+            nc.scalar.copy(
+                out=out_tiles[chunk][:, ROPED_HEADS:HEADS, j : j + GROUP, :],
+                in_=acc_tiles[group][:, :, KV_HEADS * HD :].rearrange("p t (h d) -> p h t d", d=HD),
+            )
+
+        def rope_k(group):
+            chunk, j = divmod(group * GROUP, CHUNK)
+            t = group * GROUP % TOK
+            u = acc_tiles.pop(group)[:, :, 0 : KV_HEADS * HD]
+            nc.vector.tensor_tensor(
+                out=out_tiles[chunk][:, Q_HEADS:ROPED_HEADS, j : j + GROUP, :].rearrange(
+                    "p h t d -> p t h d"
+                ),
+                in0=u.rearrange("p t (h d) -> p t h d", d=HD),
+                in1=cos_k[:, t : t + GROUP, :].unsqueeze(2).to_broadcast([P, GROUP, KV_HEADS, HD]),
+                op=ALU.mult,
+            )
+            nc.vector.tensor_tensor(
+                out=cross_tiles[group][:, :, Q_HEADS:ROPED_HEADS, :].rearrange(
+                    "p t h (i e) -> p t h i e", e=2
+                ),
+                in0=u.rearrange("p t (h i e) -> p t h i e", i=HALF, e=2)[:, :, :, :, ::-1],
+                in1=sin_k[:, t : t + GROUP, :]
+                .rearrange("p t (i e) -> p t i e", e=2)
+                .unsqueeze(2)
+                .to_broadcast([P, GROUP, KV_HEADS, HALF, 2]),
+                op=ALU.mult,
+            )
+
+        def rope_q(n, part):
             chunk, j = divmod(n, CHUNK)
-            if j == 0:
+            group, g = divmod(n, GROUP)
+            t = n % TOK
+            if j == 0 and part == 0:
                 out_sb = out_pool.tile([P, HEADS, CHUNK, HD], F32)
                 out_tiles[chunk] = out_sb
-            nc.scalar.copy(
-                out=out_tiles[chunk][:, ROPED_HEADS:HEADS, j, :],
-                in_=acc_tiles[n, 2][:, KV_HEADS * HD :].rearrange("p (h d) -> p h d", d=HD),
-            )
-
-        def straight_product(u, heads, cos_row, out):
+            if g == 0 and part == 0:
+                cross = cross_pool.tile([P, GROUP, ROPED_HEADS, HD], F32)
+                cross_tiles[group] = cross
+            heads = slice(part * BANK_HEADS, (part + 1) * BANK_HEADS)
+            u = acc_tiles.pop((n, part))[:]
             nc.vector.tensor_tensor(
-                out=out,
+                out=out_tiles[chunk][:, heads, j, :],
                 in0=u.rearrange("p (h d) -> p h d", d=HD),
-                in1=cos_row.unsqueeze(1).to_broadcast([P, heads, HD]),
+                in1=cos_q[:, t, :].unsqueeze(1).to_broadcast([P, BANK_HEADS, HD]),
                 op=ALU.mult,
             )
-
-        def cross_product(u, heads, sin_row, out):
             nc.vector.tensor_tensor(
-                out=out.rearrange("p h (i e) -> p h i e", e=2),
+                out=cross_tiles[group][:, g, heads, :].rearrange("p h (i e) -> p h i e", e=2),
                 in0=u.rearrange("p (h i e) -> p h i e", i=HALF, e=2)[:, :, :, ::-1],
-                in1=sin_row.rearrange("p (i e) -> p i e", e=2)
+                in1=sin_q[:, t, :]
+                .rearrange("p (i e) -> p i e", e=2)
                 .unsqueeze(1)
-                .to_broadcast([P, heads, HALF, 2]),
+                .to_broadcast([P, BANK_HEADS, HALF, 2]),
                 op=ALU.mult,
-            )
-
-        def rope_products(n, part):
-            chunk, j = divmod(n, CHUNK)
-            t = n % TOK
-            out_sb = out_tiles[chunk]
-            if part == 2:
-                straight_product(
-                    acc_tiles[n, 2][:, 0 : KV_HEADS * HD], KV_HEADS, cos_k[:, t, :],
-                    out_sb[:, Q_HEADS:ROPED_HEADS, j, :],
-                )
-            else:
-                if part == 0:
-                    cross = work.tile([P, ROPED_HEADS, HD], F32)
-                    cross_tiles[n] = cross
-                heads = slice(part * BANK_HEADS, (part + 1) * BANK_HEADS)
-                acc = acc_tiles.pop((n, part))
-                straight_product(acc[:], BANK_HEADS, cos_q[:, t, :], out_sb[:, heads, j, :])
-                cross_product(acc[:], BANK_HEADS, sin_q[:, t, :], cross_tiles[n][:, heads, :])
-
-        def rope_partner_k(n):
-            cross_product(
-                acc_tiles.pop((n, 2))[:, 0 : KV_HEADS * HD], KV_HEADS, sin_k[:, n % TOK, :],
-                cross_tiles[n][:, Q_HEADS:ROPED_HEADS, :],
             )
 
         def add_partners(engine, n, h0, h1):
             chunk, j = divmod(n, CHUNK)
             roped = out_tiles[chunk][:, h0:h1, j, :]
-            engine.tensor_tensor(out=roped, in0=roped, in1=cross_tiles[n][:, h0:h1, :], op=ALU.add)
+            partners = cross_tiles[n // GROUP][:, n % GROUP, h0:h1, :]
+            engine.tensor_tensor(out=roped, in0=roped, in1=partners, op=ALU.add)
 
         def store(n0, n1, h0, h1):
             chunk, j0 = divmod(n0, CHUNK)
@@ -348,16 +360,14 @@ def tile_block_pa_t_kernel(
                     )
 
         def finish(n):
-            rope_partner_k(n)
             if n < TILES - 1:
                 add_partners(nc.gpsimd, n, 0, ROPED_HEADS)
-                if n < TILES - CHUNK:
-                    if n % CHUNK == CHUNK - 1:
-                        store(n - CHUNK + 1, n + 1, 0, HEADS)
-                elif n % GROUP == 0:
+                if n >= TILES - GROUP:
                     store(n, n + 1, 0, HEADS)
-                else:
-                    store(n, n + 1, 0, HEADS)
+                elif n >= TILES - 2 * CHUNK and n % GROUP == GROUP - 1:
+                    store(n - GROUP + 1, n + 1, 0, HEADS)
+                elif n < TILES - 2 * CHUNK and n % CHUNK == CHUNK - 1:
+                    store(n - CHUNK + 1, n + 1, 0, HEADS)
             else:
                 store(n, n + 1, ROPED_HEADS, HEADS)
                 for h0, h1 in ((0, BANK_HEADS), (BANK_HEADS, Q_HEADS), (Q_HEADS, ROPED_HEADS)):
@@ -367,55 +377,54 @@ def tile_block_pa_t_kernel(
         def exists(n):
             return 0 <= n < TILES
 
-        w_work = {
-            -7: ((group_w, 0, 0), (group_w, 0, 1)),
-            -5: ((quantise_w, 0, 0), (quantise_w, 0, 1)),
-            -4: ((group_w, 1, 0), (group_w, 1, 1)),
-            -3: ((quantise_w, 1, 0), (quantise_w, 1, 1), (group_w, 2, 0)),
-            -2: ((group_w, 2, 1),),
-            -1: ((quantise_w, 2, 0), (quantise_w, 2, 1)),
+        w_jobs = {
+            -5: ((group_w, 0, 0), (group_w, 0, 1)),
+            -4: ((quantise_w, 0, 0), (quantise_w, 0, 1)),
+            -3: ((group_w, 1, 0), (group_w, 1, 1), (quantise_w, 1, 0)),
+            -2: ((quantise_w, 1, 1), (group_w, 2, 0)),
+            -1: ((group_w, 2, 1), (quantise_w, 2, 0), (quantise_w, 2, 1)),
         }
 
         with tc.manual_schedule():
             make_gain_diag()
-            for step in range(-7, TILES):
+            for step in range(-6, TILES):
                 odd = step % GROUP == 1
                 if odd and exists(step + 1):
                     quantise_x((step + 1) // GROUP)
-                if odd and exists(step - 1):
+                if odd and exists(step):
+                    copy_v(step // GROUP)
+                if odd and exists(step):
+                    rope_k(step // GROUP)
                     finish(step - 1)
                 if exists(step + 5):
                     transpose_raw(step + 5)
                 if exists(step + 3):
                     transpose_words(step + 3)
-                if exists(step):
-                    copy_v(step)
                 if exists(step + 4):
                     scale(step + 4, 0)
                 if exists(step + 5):
                     copy_raw(step + 5)
                 if exists(step):
-                    rope_products(step, 0)
+                    rope_q(step, 0)
                 if exists(step + 3):
                     group_x(step + 3)
                 if exists(step + 1):
                     multiply(step + 1, 0)
                 if exists(step + 4):
                     multiply_gain(step + 4, 1)
+                if exists(step + 4):
                     scale(step + 4, 1)
-                if exists(step + 7):
-                    square(step + 7)
-                for job, part, c in w_work.get(step, ()):
+                if exists(step + 6):
+                    square(step + 6)
+                for job, part, c in w_jobs.get(step, ()):
                     job(part, c)
-                if odd and exists(step + 5):
-                    invert((step + 5) // GROUP)
-                if step == -1:
+                if step == -2:
                     make_rope_tables()
                 if exists(step):
-                    rope_products(step, 1)
-                    rope_products(step, 2)
+                    rope_q(step, 1)
                 if exists(step + 1):
                     multiply(step + 1, 1)
+                if exists(step + 1):
                     multiply(step + 1, 2)
                 if exists(step + 5):
                     multiply_gain(step + 5, 0)

@@ -54,13 +54,15 @@ def tile_block_pa_t_kernel(
 
     with ExitStack() as ctx:
         const = ctx.enter_context(tc.tile_pool(name="const", bufs=1))
-        x_pool = ctx.enter_context(tc.tile_pool(name="x_pool", bufs=14))
+        w_pool = ctx.enter_context(tc.tile_pool(name="w_pool", bufs=PASSES * len(PARTS)))
+        x_pool = ctx.enter_context(tc.tile_pool(name="x_pool", bufs=13))
         stat = ctx.enter_context(tc.tile_pool(name="stat", bufs=3))
         work = ctx.enter_context(tc.tile_pool(name="work", bufs=3))
         cross_pool = ctx.enter_context(tc.tile_pool(name="cross_pool", bufs=2))
         out_pool = ctx.enter_context(tc.tile_pool(name="out_pool", bufs=3))
         flip_psum = ctx.enter_context(tc.psum_pool(name="flip_psum", bufs=1))
-        q_psum = ctx.enter_context(tc.psum_pool(name="q_psum", bufs=4))
+        product_psum = ctx.enter_context(tc.psum_pool(name="product_psum", bufs=PASSES))
+        q_psum = ctx.enter_context(tc.psum_pool(name="q_psum", bufs=3))
         kv_psum = ctx.enter_context(tc.psum_pool(name="kv_psum", bufs=1))
 
         x_tiles = {}
@@ -93,12 +95,14 @@ def tile_block_pa_t_kernel(
                     load_w(0, j)
             x_tiles[group] = x_sb
 
-        w_raw = const.tile([P, PASSES, PACK, N_OUT], BF16)
+        w_raw_tiles = {}
         w_rows = wqkv.rearrange("(c p j) n -> p c j n", p=P, j=PACK)
 
         def load_w(part, c):
             n0, n1 = PARTS[part]
-            nc.sync.dma_start(out=w_raw[:, c, :, n0:n1], in_=w_rows[:, c, :, n0:n1])
+            w_raw = w_pool.tile([P, PACK, n1 - n0], BF16)
+            nc.sync.dma_start(out=w_raw[:], in_=w_rows[:, c, :, n0:n1])
+            w_raw_tiles[part, c] = w_raw
 
         load_x(0)
         load_x(1)
@@ -160,7 +164,7 @@ def tile_block_pa_t_kernel(
             n0, n1 = PARTS[part]
             nc.vector.tensor_copy(
                 out=w_grouped[:, c, n0:n1, :].rearrange("p (m i) j -> p m j i", i=4),
-                in_=w_raw[:, c, :, n0:n1].rearrange("p j (m i) -> p m j i", i=4),
+                in_=w_raw_tiles[part, c][:].rearrange("p j (m i) -> p m j i", i=4),
             )
 
         def quantise_w(part, c):
@@ -205,7 +209,7 @@ def tile_block_pa_t_kernel(
             flipped_tiles[n] = flipped
 
         def multiply_gain(n, c):
-            product = flip_psum.tile([P, BANK], F32)
+            product = product_psum.tile([P, BANK], F32)
             for i in range(PASS_BLOCKS):
                 kb = c * PASS_BLOCKS + i
                 nc.tensor.matmul(
@@ -362,17 +366,14 @@ def tile_block_pa_t_kernel(
         def finish(n):
             if n < TILES - 1:
                 add_partners(nc.gpsimd, n, 0, ROPED_HEADS)
-                if n >= TILES - GROUP:
-                    store(n, n + 1, 0, HEADS)
-                elif n >= TILES - 2 * CHUNK and n % GROUP == GROUP - 1:
-                    store(n - GROUP + 1, n + 1, 0, HEADS)
-                elif n < TILES - 2 * CHUNK and n % CHUNK == CHUNK - 1:
-                    store(n - CHUNK + 1, n + 1, 0, HEADS)
+                size = CHUNK if n < TILES - 2 * CHUNK else GROUP
+                if n % size == size - 1:
+                    store(n - size + 1, n + 1, 0, HEADS)
             else:
-                store(n, n + 1, ROPED_HEADS, HEADS)
-                for h0, h1 in ((0, BANK_HEADS), (BANK_HEADS, Q_HEADS), (Q_HEADS, ROPED_HEADS)):
+                store(n - GROUP + 1, n + 1, ROPED_HEADS, HEADS)
+                for h0, h1 in ((Q_HEADS, ROPED_HEADS), (0, BANK_HEADS), (BANK_HEADS, Q_HEADS)):
                     add_partners(nc.vector, n, h0, h1)
-                    store(n, n + 1, h0, h1)
+                    store(n - GROUP + 1, n + 1, h0, h1)
 
         def exists(n):
             return 0 <= n < TILES
@@ -381,13 +382,12 @@ def tile_block_pa_t_kernel(
             -5: ((group_w, 0, 0), (group_w, 0, 1)),
             -4: ((quantise_w, 0, 0), (quantise_w, 0, 1)),
             -3: ((group_w, 1, 0), (group_w, 1, 1), (quantise_w, 1, 0)),
-            -2: ((quantise_w, 1, 1), (group_w, 2, 0)),
-            -1: ((group_w, 2, 1), (quantise_w, 2, 0), (quantise_w, 2, 1)),
+            -2: ((quantise_w, 1, 1), (group_w, 2, 0), (group_w, 2, 1), (quantise_w, 2, 0), (quantise_w, 2, 1)),
         }
 
         with tc.manual_schedule():
             make_gain_diag()
-            for step in range(-6, TILES):
+            for step in range(-5, TILES):
                 odd = step % GROUP == 1
                 if odd and exists(step + 1):
                     quantise_x((step + 1) // GROUP)
@@ -396,12 +396,16 @@ def tile_block_pa_t_kernel(
                 if odd and exists(step):
                     rope_k(step // GROUP)
                     finish(step - 1)
-                if exists(step + 5):
-                    transpose_raw(step + 5)
                 if exists(step + 3):
                     transpose_words(step + 3)
+                if exists(step + 5):
+                    transpose_raw(step + 5)
+                if exists(step + 5):
+                    square(step + 5)
                 if exists(step + 4):
                     scale(step + 4, 0)
+                if exists(step + 4):
+                    scale(step + 4, 1)
                 if exists(step + 5):
                     copy_raw(step + 5)
                 if exists(step):
@@ -410,23 +414,18 @@ def tile_block_pa_t_kernel(
                     group_x(step + 3)
                 if exists(step + 1):
                     multiply(step + 1, 0)
-                if exists(step + 4):
-                    multiply_gain(step + 4, 1)
-                if exists(step + 4):
-                    scale(step + 4, 1)
-                if exists(step + 6):
-                    square(step + 6)
                 for job, part, c in w_jobs.get(step, ()):
                     job(part, c)
-                if step == -2:
+                if step == -1:
                     make_rope_tables()
                 if exists(step):
                     rope_q(step, 1)
                 if exists(step + 1):
-                    multiply(step + 1, 1)
-                if exists(step + 1):
                     multiply(step + 1, 2)
                 if exists(step + 5):
                     multiply_gain(step + 5, 0)
+                    multiply_gain(step + 5, 1)
+                if exists(step + 1):
+                    multiply(step + 1, 1)
                 if odd and exists(step):
                     finish(step)

@@ -245,7 +245,7 @@ def tile_block_pa_t_kernel(
                 grouped_tiles[group] = grouped
             out = grouped_tiles[group][:, j].rearrange("p c r j -> p (c r j)").bitcast(F32)
             source = word_tiles.pop(n)[:].rearrange("p c u r -> p c r u")
-            if n % 4 != 0:
+            if n % 4 != 0 or n < 4:
                 nc.vector.tensor_copy(out=out, in_=source)
             else:
                 nc.scalar.copy(out=out, in_=source)
@@ -291,10 +291,10 @@ def tile_block_pa_t_kernel(
                 in_=acc_tiles[group][:, :, KV_HEADS * HD :].rearrange("p t (h d) -> p h t d", d=HD),
             )
 
-        def rope_k(group):
+        def rope_k_straight(group):
             chunk, j = divmod(group * GROUP, CHUNK)
             t = group * GROUP % TOK
-            u = acc_tiles.pop(group)[:, :, 0 : KV_HEADS * HD]
+            u = acc_tiles[group][:, :, 0 : KV_HEADS * HD]
             nc.vector.tensor_tensor(
                 out=out_tiles[chunk][:, Q_HEADS:ROPED_HEADS, j : j + GROUP, :].rearrange(
                     "p h t d -> p t h d"
@@ -303,6 +303,10 @@ def tile_block_pa_t_kernel(
                 in1=cos_k[:, t : t + GROUP, :].unsqueeze(2).to_broadcast([P, GROUP, KV_HEADS, HD]),
                 op=ALU.mult,
             )
+
+        def rope_k_cross(group):
+            t = group * GROUP % TOK
+            u = acc_tiles.pop(group)[:, :, 0 : KV_HEADS * HD]
             nc.vector.tensor_tensor(
                 out=cross_tiles[group][:, :, Q_HEADS:ROPED_HEADS, :].rearrange(
                     "p t h (i e) -> p t h i e", e=2
@@ -387,44 +391,46 @@ def tile_block_pa_t_kernel(
 
         with tc.manual_schedule():
             make_gain_diag()
-            for step in range(-5, TILES):
+            for step in range(-6, TILES):
                 odd = step % GROUP == 1
                 if odd and exists(step + 1):
                     quantise_x((step + 1) // GROUP)
                 if odd and exists(step):
                     copy_v(step // GROUP)
                 if odd and exists(step):
-                    rope_k(step // GROUP)
+                    rope_k_straight(step // GROUP)
+                if odd and exists(step):
+                    rope_k_cross(step // GROUP)
                     finish(step - 1)
                 if exists(step + 3):
                     transpose_words(step + 3)
-                if exists(step + 5):
-                    transpose_raw(step + 5)
+                if exists(step + 4):
+                    multiply_gain(step + 4, 0)
+                    multiply_gain(step + 4, 1)
                 if exists(step + 5):
                     square(step + 5)
-                if exists(step + 4):
-                    scale(step + 4, 0)
-                if exists(step + 4):
-                    scale(step + 4, 1)
                 if exists(step + 5):
                     copy_raw(step + 5)
                 if exists(step):
                     rope_q(step, 0)
-                if exists(step + 3):
-                    group_x(step + 3)
-                if exists(step + 1):
-                    multiply(step + 1, 0)
                 for job, part, c in w_jobs.get(step, ()):
                     job(part, c)
                 if step == -1:
                     make_rope_tables()
+                if exists(step + 3):
+                    group_x(step + 3)
+                if exists(step + 1):
+                    multiply(step + 1, 0)
+                if exists(step + 4):
+                    scale(step + 4, 0)
+                if exists(step + 4):
+                    scale(step + 4, 1)
                 if exists(step):
                     rope_q(step, 1)
                 if exists(step + 1):
                     multiply(step + 1, 2)
-                if exists(step + 5):
-                    multiply_gain(step + 5, 0)
-                    multiply_gain(step + 5, 1)
+                if exists(step + 6):
+                    transpose_raw(step + 6)
                 if exists(step + 1):
                     multiply(step + 1, 1)
                 if odd and exists(step):

@@ -245,7 +245,7 @@ def tile_block_pa_t_kernel(
                 grouped_tiles[group] = grouped
             out = grouped_tiles[group][:, j].rearrange("p c r j -> p (c r j)").bitcast(F32)
             source = word_tiles.pop(n)[:].rearrange("p c u r -> p c r u")
-            if n % 4 != 0 or n < 4:
+            if n < 4 or n % 2 == 1 or n % 8 == 2:
                 nc.vector.tensor_copy(out=out, in_=source)
             else:
                 nc.scalar.copy(out=out, in_=source)
@@ -391,17 +391,17 @@ def tile_block_pa_t_kernel(
 
         with tc.manual_schedule():
             make_gain_diag()
-            for step in range(-6, TILES):
+            for step in range(-5, TILES):
                 odd = step % GROUP == 1
-                if odd and exists(step + 1):
-                    quantise_x((step + 1) // GROUP)
-                if odd and exists(step):
-                    copy_v(step // GROUP)
                 if odd and exists(step):
                     rope_k_straight(step // GROUP)
                 if odd and exists(step):
                     rope_k_cross(step // GROUP)
                     finish(step - 1)
+                if odd and exists(step + 1):
+                    quantise_x((step + 1) // GROUP)
+                if exists(step + 5):
+                    transpose_raw(step + 5)
                 if exists(step + 3):
                     transpose_words(step + 3)
                 if exists(step + 4):
@@ -429,8 +429,8 @@ def tile_block_pa_t_kernel(
                     rope_q(step, 1)
                 if exists(step + 1):
                     multiply(step + 1, 2)
-                if exists(step + 6):
-                    transpose_raw(step + 6)
+                if not odd and exists(step + 1):
+                    copy_v((step + 1) // GROUP)
                 if exists(step + 1):
                     multiply(step + 1, 1)
                 if odd and exists(step):

@@ -239,30 +239,28 @@ def tile_block_pa_t_kernel(
             word_tiles[n] = words
 
         def group_x(n):
-            group, j = divmod(n, GROUP)
-            if j == 0:
-                grouped = work.tile([P, GROUP, PASSES, P, PACK], BF16, align_bytes=64)
-                grouped_tiles[group] = grouped
-            out = grouped_tiles[group][:, j].rearrange("p c r j -> p (c r j)").bitcast(F32)
+            grouped = work.tile([P, PASSES, P, PACK], BF16, align_bytes=64)
+            out = grouped[:].rearrange("p c r j -> p (c r j)").bitcast(F32)
             source = word_tiles.pop(n)[:].rearrange("p c u r -> p c r u")
-            if n < 4 or n % 2 == 1 or n % 8 == 2:
+            if n < 4 or n % 4 != 0 and n < TILES - CHUNK:
                 nc.vector.tensor_copy(out=out, in_=source)
             else:
                 nc.scalar.copy(out=out, in_=source)
+            grouped_tiles[n] = grouped
 
-        def quantise_x(group):
-            codes = work.tile([P, GROUP, PASSES, P], U32, align_bytes=64)
-            scales = work.tile([P, GROUP, PASSES, P], U8, align_bytes=64)
+        def quantise_x(n):
+            codes = work.tile([P, PASSES, P], U32, align_bytes=64)
+            scales = work.tile([P, PASSES, P], U8, align_bytes=64)
             nc.vector.quantize_mx(
-                out=codes[:].rearrange("p g c r -> p (g c r)").bitcast(FP8X4),
-                scales=scales[:].rearrange("p g c r -> p (g c r)"),
-                in_=grouped_tiles.pop(group)[:].rearrange("p g c r j -> p (g c r j)"),
+                out=codes[:].rearrange("p c r -> p (c r)").bitcast(FP8X4),
+                scales=scales[:].rearrange("p c r -> p (c r)"),
+                in_=grouped_tiles.pop(n)[:].rearrange("p c r j -> p (c r j)"),
             )
-            code_tiles[group] = (codes, scales)
+            code_tiles[n] = (codes, scales)
 
         def multiply(n, part):
             group, j = divmod(n, GROUP)
-            codes, scales = code_tiles[group]
+            codes, scales = code_tiles[n]
             n0, n1 = PARTS[part]
             if part < 2:
                 q_acc = q_psum.tile([P, BANK], F32)
@@ -276,8 +274,8 @@ def tile_block_pa_t_kernel(
             for c in range(PASSES):
                 nc.tensor.matmul_mx(
                     out=acc,
-                    lhsT=codes[:, j, c, :].bitcast(FP8X4),
-                    lhsT_scale=scales[:, j, c, :],
+                    lhsT=codes[:, c, :].bitcast(FP8X4),
+                    lhsT_scale=scales[:, c, :],
                     rhs=w_codes[:, c, n0:n1].bitcast(FP8X4),
                     rhs_scale=w_scales[:, c, n0:n1],
                     start=(c == 0),
@@ -383,48 +381,48 @@ def tile_block_pa_t_kernel(
             return 0 <= n < TILES
 
         w_jobs = {
-            -5: ((group_w, 0, 0), (group_w, 0, 1)),
-            -4: ((quantise_w, 0, 0), (quantise_w, 0, 1)),
-            -3: ((group_w, 1, 0), (group_w, 1, 1), (quantise_w, 1, 0)),
-            -2: ((quantise_w, 1, 1), (group_w, 2, 0), (group_w, 2, 1), (quantise_w, 2, 0), (quantise_w, 2, 1)),
+            -4: ((group_w, 0, 0), (group_w, 0, 1), (quantise_w, 0, 0), (quantise_w, 0, 1)),
+            -3: ((group_w, 1, 0),),
+            -2: ((group_w, 1, 1), (quantise_w, 1, 0), (quantise_w, 1, 1)),
+            -1: ((group_w, 2, 0), (group_w, 2, 1), (quantise_w, 2, 0), (quantise_w, 2, 1)),
         }
 
         with tc.manual_schedule():
             make_gain_diag()
-            for step in range(-5, TILES):
+            for step in range(-4, TILES):
                 odd = step % GROUP == 1
                 if odd and exists(step):
                     rope_k_straight(step // GROUP)
                 if odd and exists(step):
                     rope_k_cross(step // GROUP)
                     finish(step - 1)
-                if odd and exists(step + 1):
-                    quantise_x((step + 1) // GROUP)
-                if exists(step + 5):
-                    transpose_raw(step + 5)
-                if exists(step + 3):
-                    transpose_words(step + 3)
+                if exists(step + 1):
+                    quantise_x(step + 1)
                 if exists(step + 4):
-                    multiply_gain(step + 4, 0)
-                    multiply_gain(step + 4, 1)
-                if exists(step + 5):
-                    square(step + 5)
-                if exists(step + 5):
-                    copy_raw(step + 5)
+                    transpose_raw(step + 4)
+                if exists(step + 2):
+                    transpose_words(step + 2)
+                if exists(step + 3):
+                    multiply_gain(step + 3, 0)
+                    multiply_gain(step + 3, 1)
+                if exists(step + 4):
+                    square(step + 4)
+                if exists(step + 4):
+                    copy_raw(step + 4)
                 if exists(step):
                     rope_q(step, 0)
+                if exists(step + 2):
+                    group_x(step + 2)
+                if exists(step + 1):
+                    multiply(step + 1, 0)
+                if exists(step + 3):
+                    scale(step + 3, 0)
+                if exists(step + 3):
+                    scale(step + 3, 1)
                 for job, part, c in w_jobs.get(step, ()):
                     job(part, c)
                 if step == -1:
                     make_rope_tables()
-                if exists(step + 3):
-                    group_x(step + 3)
-                if exists(step + 1):
-                    multiply(step + 1, 0)
-                if exists(step + 4):
-                    scale(step + 4, 0)
-                if exists(step + 4):
-                    scale(step + 4, 1)
                 if exists(step):
                     rope_q(step, 1)
                 if exists(step + 1):

@@ -108,13 +108,13 @@ def tile_block_pa_t_kernel(
         load_x(1)
         load_w(1, 0)
         load_w(1, 1)
+        load_w(2, 0)
+        load_w(2, 1)
         load_x(2)
         cos_q = const.tile([P, TOK, HD], BF16)
         nc.sync.dma_start(out=cos_q[:], in_=rope_cos.rearrange("(p t) d -> p t d", t=TOK))
         sin_raw = const.tile([P, TOK, HD], BF16)
         nc.sync.dma_start(out=sin_raw[:], in_=rope_sin.rearrange("(p t) d -> p t d", t=TOK))
-        load_w(2, 0)
-        load_w(2, 1)
         for group in range(3, TILES // GROUP):
             load_x(group)
 
@@ -156,8 +156,9 @@ def tile_block_pa_t_kernel(
                 op=ALU.mult,
             )
             for k_table, q_table in ((sin_k, sin_q), (cos_k, cos_q)):
-                nc.vector.tensor_scalar(
-                    out=k_table[:], in0=q_table[:], scalar1=HD**-0.5, scalar2=None, op0=ALU.mult
+                nc.gpsimd.tensor_scalar(
+                    out=k_table[:], in0=q_table[:], scalar1=HD**-0.5, scalar2=0.0,
+                    op0=ALU.mult, op1=ALU.add,
                 )
 
         def group_w(part, c):
@@ -367,7 +368,9 @@ def tile_block_pa_t_kernel(
 
         def finish(n):
             if n < TILES - 1:
-                add_partners(nc.gpsimd, n, 0, ROPED_HEADS)
+                bounds = (0, BANK_HEADS, ROPED_HEADS) if n == TILES - GROUP else (0, ROPED_HEADS)
+                for h0, h1 in zip(bounds, bounds[1:]):
+                    add_partners(nc.gpsimd, n, h0, h1)
                 size = CHUNK if n < TILES - 2 * CHUNK else GROUP
                 if n % size == size - 1:
                     store(n - size + 1, n + 1, 0, HEADS)
@@ -383,8 +386,8 @@ def tile_block_pa_t_kernel(
         w_jobs = {
             -4: ((group_w, 0, 0), (group_w, 0, 1), (quantise_w, 0, 0), (quantise_w, 0, 1)),
             -3: ((group_w, 1, 0),),
-            -2: ((group_w, 1, 1), (quantise_w, 1, 0), (quantise_w, 1, 1)),
-            -1: ((group_w, 2, 0), (group_w, 2, 1), (quantise_w, 2, 0), (quantise_w, 2, 1)),
+            -2: ((group_w, 1, 1), (quantise_w, 1, 0), (quantise_w, 1, 1), (group_w, 2, 0)),
+            -1: ((group_w, 2, 1), (quantise_w, 2, 0), (quantise_w, 2, 1)),
         }
 
         with tc.manual_schedule():
@@ -405,6 +408,9 @@ def tile_block_pa_t_kernel(
                 if exists(step + 3):
                     multiply_gain(step + 3, 0)
                     multiply_gain(step + 3, 1)
+                if step == 0:
+                    multiply(0, 1)
+                    multiply(0, 2)
                 if exists(step + 4):
                     square(step + 4)
                 if exists(step + 4):
@@ -415,8 +421,12 @@ def tile_block_pa_t_kernel(
                     group_x(step + 2)
                 if exists(step + 1):
                     multiply(step + 1, 0)
+                if exists(step + 1) and step >= 0:
+                    multiply(step + 1, 2)
                 if exists(step + 3):
                     scale(step + 3, 0)
+                if not odd and exists(step + 1):
+                    copy_v((step + 1) // GROUP)
                 if exists(step + 3):
                     scale(step + 3, 1)
                 for job, part, c in w_jobs.get(step, ()):
@@ -425,11 +435,7 @@ def tile_block_pa_t_kernel(
                     make_rope_tables()
                 if exists(step):
                     rope_q(step, 1)
-                if exists(step + 1):
-                    multiply(step + 1, 2)
-                if not odd and exists(step + 1):
-                    copy_v((step + 1) // GROUP)
-                if exists(step + 1):
+                if exists(step + 1) and step >= 0:
                     multiply(step + 1, 1)
                 if odd and exists(step):
                     finish(step)

@@ -386,8 +386,8 @@ def tile_block_pa_t_kernel(
         w_jobs = {
             -4: ((group_w, 0, 0), (group_w, 0, 1), (quantise_w, 0, 0), (quantise_w, 0, 1)),
             -3: ((group_w, 1, 0),),
-            -2: ((group_w, 1, 1), (quantise_w, 1, 0), (quantise_w, 1, 1), (group_w, 2, 0)),
-            -1: ((group_w, 2, 1), (quantise_w, 2, 0), (quantise_w, 2, 1)),
+            -2: ((group_w, 1, 1), (quantise_w, 1, 0), (quantise_w, 1, 1)),
+            -1: ((group_w, 2, 0), (group_w, 2, 1), (quantise_w, 2, 0), (quantise_w, 2, 1)),
         }
 
         with tc.manual_schedule():
@@ -419,10 +419,10 @@ def tile_block_pa_t_kernel(
                     rope_q(step, 0)
                 if exists(step + 2):
                     group_x(step + 2)
-                if exists(step + 1):
-                    multiply(step + 1, 0)
                 if exists(step + 1) and step >= 0:
                     multiply(step + 1, 2)
+                if exists(step + 1):
+                    multiply(step + 1, 0)
                 if exists(step + 3):
                     scale(step + 3, 0)
                 if not odd and exists(step + 1):

from contextlib import ExitStack

import concourse.mybir as mybir
from concourse.masks import make_identity

F32 = mybir.dt.float32
BF16 = mybir.dt.bfloat16
U32 = mybir.dt.uint32
U8 = mybir.dt.uint8
FP8X4 = mybir.dt.float8_e4m3fn_x4
ALU = mybir.AluOpType
ACT = mybir.ActivationFunctionType

P = 128
BATCH = 2
SEQ = 2048
D = 1024
HD = 64
HALF = HD // 2
Q_HEADS = 16
KV_HEADS = 2
ROPED_HEADS = Q_HEADS + KV_HEADS
HEADS = Q_HEADS + 2 * KV_HEADS
N_OUT = HEADS * HD
EPS = 1e-5

PACK = 4
K_PASS = P * PACK
PASSES = D // K_PASS
PAIRS = PACK // 2
K_BLOCKS = D // P
PASS_BLOCKS = K_BLOCKS // PASSES

TOK = SEQ // P
TILES = BATCH * TOK
GROUP = 2
CHUNK = 4
BANK = 512
BANK_HEADS = BANK // HD
PARTS = ((0, 512), (512, 1024), (1024, N_OUT))

FLOPS = 2 * BATCH * SEQ * D * N_OUT


def tile_block_pa_t_kernel(
    tc, x, norm1_w, wqkv, rope_sin, rope_cos, out_0, out_1, out_2
):
    nc = tc.nc

    x_view = x.rearrange("b (p t) k -> b p t k", t=TOK)
    q_view = out_0.rearrange("b r g (p t) d -> b p (r g) t d", t=TOK)
    k_view = out_1.rearrange("b g (p t) d -> b p g t d", t=TOK)
    v_view = out_2.rearrange("b g (p t) d -> b p g t d", t=TOK)

    with ExitStack() as ctx:
        const = ctx.enter_context(tc.tile_pool(name="const", bufs=1))
        w_pool = ctx.enter_context(tc.tile_pool(name="w_pool", bufs=PASSES * len(PARTS)))
        x_pool = ctx.enter_context(tc.tile_pool(name="x_pool", bufs=13))
        stat = ctx.enter_context(tc.tile_pool(name="stat", bufs=3))
        work = ctx.enter_context(tc.tile_pool(name="work", bufs=3))
        cross_pool = ctx.enter_context(tc.tile_pool(name="cross_pool", bufs=2))
        out_pool = ctx.enter_context(tc.tile_pool(name="out_pool", bufs=3))
        flip_psum = ctx.enter_context(tc.psum_pool(name="flip_psum", bufs=1))
        product_psum = ctx.enter_context(tc.psum_pool(name="product_psum", bufs=PASSES))
        q_psum = ctx.enter_context(tc.psum_pool(name="q_psum", bufs=3))
        kv_psum = ctx.enter_context(tc.psum_pool(name="kv_psum", bufs=1))

        x_tiles = {}
        sum_tiles = {}
        rstd_tiles = {}
        raw_tiles = {}
        flipped_tiles = {}
        product_tiles = {}
        xn_tiles = {}
        word_tiles = {}
        grouped_tiles = {}
        code_tiles = {}
        acc_tiles = {}
        cross_tiles = {}
        out_tiles = {}

        gain_rows = const.tile([P, P], BF16)
        nc.vector.memset(gain_rows[:], 0.0)
        nc.sync.dma_start(out=gain_rows[0:K_BLOCKS, :], in_=norm1_w.rearrange("(kb i) -> kb i", i=P))

        def load_x(group):
            b, t0 = divmod(group * GROUP, TOK)
            x_sb = x_pool.tile([P, GROUP, D], BF16)
            size = 1 if group == 0 else GROUP
            for j in range(0, GROUP, size):
                nc.sync.dma_start(
                    out=x_sb[:, j : j + size, :], in_=x_view[b, :, t0 + j : t0 + j + size, :]
                )
                if group == 0:
                    load_w(0, j)
            x_tiles[group] = x_sb

        w_raw_tiles = {}
        w_rows = wqkv.rearrange("(c p j) n -> p c j n", p=P, j=PACK)

        def load_w(part, c):
            n0, n1 = PARTS[part]
            w_raw = w_pool.tile([P, PACK, n1 - n0], BF16)
            nc.sync.dma_start(out=w_raw[:], in_=w_rows[:, c, :, n0:n1])
            w_raw_tiles[part, c] = w_raw

        load_x(0)
        load_x(1)
        load_w(1, 0)
        load_w(1, 1)
        load_w(2, 0)
        load_w(2, 1)
        load_x(2)
        cos_q = const.tile([P, TOK, HD], BF16)
        nc.sync.dma_start(out=cos_q[:], in_=rope_cos.rearrange("(p t) d -> p t d", t=TOK))
        sin_raw = const.tile([P, TOK, HD], BF16)
        nc.sync.dma_start(out=sin_raw[:], in_=rope_sin.rearrange("(p t) d -> p t d", t=TOK))
        for group in range(3, TILES // GROUP):
            load_x(group)

        eps = const.tile([P, 1], F32)
        nc.vector.memset(eps[:], EPS)
        warm = const.tile([P, 1], F32)
        nc.scalar.activation(out=warm[:], in_=eps[:], func=ACT.Abs_reciprocal_sqrt)
        ident_bf = const.tile([P, P], BF16)
        make_identity(nc, ident_bf[:])
        ident = const.tile([P, P], F32)
        make_identity(nc, ident[:])
        signs = const.tile([P, HALF, 2], BF16)
        nc.vector.memset(signs[:, :, 0], -1.0)
        nc.vector.memset(signs[:, :, 1], 1.0)

        w_grouped = const.tile([P, PASSES, N_OUT, PACK], BF16, align_bytes=64)
        w_codes = const.tile([P, PASSES, N_OUT], U32, align_bytes=64)
        w_scales = const.tile([P, PASSES, N_OUT], U8, align_bytes=64)
        gain_diag = const.tile([P, K_BLOCKS, P], BF16)
        sin_q = const.tile([P, TOK, HD], BF16)
        sin_k = const.tile([P, TOK, HD], BF16)
        cos_k = const.tile([P, TOK, HD], BF16)

        def make_gain_diag():
            raw = flip_psum.tile([P, K_BLOCKS, P], BF16)
            nc.tensor.transpose(raw[:, 0, :], gain_rows[:], ident_bf[:])
            gain_columns = const.tile([P, K_BLOCKS], F32)
            nc.vector.tensor_copy(out=gain_columns[:], in_=raw[:, 0, 0:K_BLOCKS])
            for kb in range(K_BLOCKS):
                nc.vector.tensor_scalar(
                    out=gain_diag[:, kb, :], in0=ident_bf[:], scalar1=gain_columns[:, kb : kb + 1],
                    scalar2=None, op0=ALU.mult,
                )

        def make_rope_tables():
            nc.vector.tensor_tensor(
                out=sin_q[:], in0=sin_raw[:],
                in1=signs[:].rearrange("p i e -> p (i e)").unsqueeze(1).to_broadcast([P, TOK, HD]),
                op=ALU.mult,
            )
            for k_table, q_table in ((sin_k, sin_q), (cos_k, cos_q)):
                nc.gpsimd.tensor_scalar(
                    out=k_table[:], in0=q_table[:], scalar1=HD**-0.5, scalar2=0.0,
                    op0=ALU.mult, op1=ALU.add,
                )

        def group_w(part, c):
            n0, n1 = PARTS[part]
            nc.vector.tensor_copy(
                out=w_grouped[:, c, n0:n1, :].rearrange("p (m i) j -> p m j i", i=4),
                in_=w_raw_tiles[part, c][:].rearrange("p j (m i) -> p m j i", i=4),
            )

        def quantise_w(part, c):
            n0, n1 = PARTS[part]
            nc.vector.quantize_mx(
                out=w_codes[:, c, n0:n1].bitcast(FP8X4),
                scales=w_scales[:, c, n0:n1],
                in_=w_grouped[:, c, n0:n1, :].rearrange("p n j -> p (n j)"),
            )

        def x_row(n):
            return x_tiles[n // GROUP][:, n % GROUP, :]

        def square(n):
            group, j = divmod(n, GROUP)
            if j == 0:
                sum_sq = stat.tile([P, GROUP], F32)
                sum_tiles[group] = sum_sq
            squares = work.tile([P, D], BF16)
            nc.scalar.activation(
                out=squares[:], in_=x_row(n), func=ACT.Square, accum_out=sum_tiles[group][:, j : j + 1]
            )
            if j == GROUP - 1:
                rstd = stat.tile([P, GROUP], F32)
                nc.scalar.activation(
                    out=rstd[:], in_=sum_tiles.pop(group)[:], func=ACT.Abs_reciprocal_sqrt,
                    bias=eps[:], scale=1.0 / D,
                )
                rstd_tiles[group] = rstd

        def transpose_raw(n):
            raw = flip_psum.tile([P, K_BLOCKS, P], BF16)
            for kb in range(K_BLOCKS):
                nc.tensor.transpose(raw[:, kb, :], x_row(n)[:, kb * P : (kb + 1) * P], ident_bf[:])
            raw_tiles[n] = raw

        def copy_raw(n):
            flipped = work.tile([P, K_BLOCKS, P], BF16)
            out = flipped[:].rearrange("p kb r -> p (kb r)").bitcast(F32)
            source = raw_tiles.pop(n)[:].rearrange("p kb r -> p (kb r)").bitcast(F32)
            nc.scalar.copy(out=out, in_=source)
            flipped_tiles[n] = flipped

        def multiply_gain(n, c):
            product = product_psum.tile([P, BANK], F32)
            for i in range(PASS_BLOCKS):
                kb = c * PASS_BLOCKS + i
                nc.tensor.matmul(
                    product[:, i * P : (i + 1) * P], lhsT=flipped_tiles[n][:, kb, :],
                    rhs=gain_diag[:, kb, :], start=True, stop=True,
                )
            product_tiles[n, c] = product

        def scale(n, c):
            group, j = divmod(n, GROUP)
            if c == 0:
                xn = work.tile([P, PASSES, PAIRS, P, 2], BF16)
                xn_tiles[n] = xn
            nc.scalar.activation(
                out=xn_tiles[n][:, c],
                in_=product_tiles.pop((n, c))[:].rearrange("p (i u e) -> p u i e", u=PAIRS, e=2),
                func=ACT.Copy, scale=rstd_tiles[group][:, j : j + 1],
            )

        def transpose_words(n):
            pairs = xn_tiles.pop(n)[:].rearrange("p c u i e -> p (c u i e)").bitcast(F32)
            words = flip_psum.tile([P, PASSES, PAIRS, P], F32)
            for c in range(PASSES):
                for u in range(PAIRS):
                    first = (c * PAIRS + u) * P
                    nc.tensor.transpose(words[:, c, u, :], pairs[:, first : first + P], ident[:])
            word_tiles[n] = words

        def group_x(n):
            grouped = work.tile([P, PASSES, P, PACK], BF16, align_bytes=64)
            out = grouped[:].rearrange("p c r j -> p (c r j)").bitcast(F32)
            source = word_tiles.pop(n)[:].rearrange("p c u r -> p c r u")
            if n < 4 or n % 4 != 0 and n < TILES - CHUNK:
                nc.vector.tensor_copy(out=out, in_=source)
            else:
                nc.scalar.copy(out=out, in_=source)
            grouped_tiles[n] = grouped

        def quantise_x(n):
            codes = work.tile([P, PASSES, P], U32, align_bytes=64)
            scales = work.tile([P, PASSES, P], U8, align_bytes=64)
            nc.vector.quantize_mx(
                out=codes[:].rearrange("p c r -> p (c r)").bitcast(FP8X4),
                scales=scales[:].rearrange("p c r -> p (c r)"),
                in_=grouped_tiles.pop(n)[:].rearrange("p c r j -> p (c r j)"),
            )
            code_tiles[n] = (codes, scales)

        def multiply(n, part):
            group, j = divmod(n, GROUP)
            codes, scales = code_tiles[n]
            n0, n1 = PARTS[part]
            if part < 2:
                q_acc = q_psum.tile([P, BANK], F32)
                acc_tiles[n, part] = q_acc
                acc = q_acc[:]
            else:
                if j == 0:
                    kv_acc = kv_psum.tile([P, GROUP, n1 - n0], F32)
                    acc_tiles[group] = kv_acc
                acc = acc_tiles[group][:, j, :]
            for c in range(PASSES):
                nc.tensor.matmul_mx(
                    out=acc,
                    lhsT=codes[:, c, :].bitcast(FP8X4),
                    lhsT_scale=scales[:, c, :],
                    rhs=w_codes[:, c, n0:n1].bitcast(FP8X4),
                    rhs_scale=w_scales[:, c, n0:n1],
                    start=(c == 0),
                    stop=(c == PASSES - 1),
                )

        def copy_v(group):
            chunk, j = divmod(group * GROUP, CHUNK)
            nc.scalar.copy(
                out=out_tiles[chunk][:, ROPED_HEADS:HEADS, j : j + GROUP, :],
                in_=acc_tiles[group][:, :, KV_HEADS * HD :].rearrange("p t (h d) -> p h t d", d=HD),
            )

        def rope_k_straight(group):
            chunk, j = divmod(group * GROUP, CHUNK)
            t = group * GROUP % TOK
            u = acc_tiles[group][:, :, 0 : KV_HEADS * HD]
            nc.vector.tensor_tensor(
                out=out_tiles[chunk][:, Q_HEADS:ROPED_HEADS, j : j + GROUP, :].rearrange(
                    "p h t d -> p t h d"
                ),
                in0=u.rearrange("p t (h d) -> p t h d", d=HD),
                in1=cos_k[:, t : t + GROUP, :].unsqueeze(2).to_broadcast([P, GROUP, KV_HEADS, HD]),
                op=ALU.mult,
            )

        def rope_k_cross(group):
            t = group * GROUP % TOK
            u = acc_tiles.pop(group)[:, :, 0 : KV_HEADS * HD]
            nc.vector.tensor_tensor(
                out=cross_tiles[group][:, :, Q_HEADS:ROPED_HEADS, :].rearrange(
                    "p t h (i e) -> p t h i e", e=2
                ),
                in0=u.rearrange("p t (h i e) -> p t h i e", i=HALF, e=2)[:, :, :, :, ::-1],
                in1=sin_k[:, t : t + GROUP, :]
                .rearrange("p t (i e) -> p t i e", e=2)
                .unsqueeze(2)
                .to_broadcast([P, GROUP, KV_HEADS, HALF, 2]),
                op=ALU.mult,
            )

        def rope_q(n, part):
            chunk, j = divmod(n, CHUNK)
            group, g = divmod(n, GROUP)
            t = n % TOK
            if j == 0 and part == 0:
                out_sb = out_pool.tile([P, HEADS, CHUNK, HD], F32)
                out_tiles[chunk] = out_sb
            if g == 0 and part == 0:
                cross = cross_pool.tile([P, GROUP, ROPED_HEADS, HD], F32)
                cross_tiles[group] = cross
            heads = slice(part * BANK_HEADS, (part + 1) * BANK_HEADS)
            u = acc_tiles.pop((n, part))[:]
            nc.vector.tensor_tensor(
                out=out_tiles[chunk][:, heads, j, :],
                in0=u.rearrange("p (h d) -> p h d", d=HD),
                in1=cos_q[:, t, :].unsqueeze(1).to_broadcast([P, BANK_HEADS, HD]),
                op=ALU.mult,
            )
            nc.vector.tensor_tensor(
                out=cross_tiles[group][:, g, heads, :].rearrange("p h (i e) -> p h i e", e=2),
                in0=u.rearrange("p (h i e) -> p h i e", i=HALF, e=2)[:, :, :, ::-1],
                in1=sin_q[:, t, :]
                .rearrange("p (i e) -> p i e", e=2)
                .unsqueeze(1)
                .to_broadcast([P, BANK_HEADS, HALF, 2]),
                op=ALU.mult,
            )

        def add_partners(engine, n, h0, h1):
            chunk, j = divmod(n, CHUNK)
            roped = out_tiles[chunk][:, h0:h1, j, :]
            partners = cross_tiles[n // GROUP][:, n % GROUP, h0:h1, :]
            engine.tensor_tensor(out=roped, in0=roped, in1=partners, op=ALU.add)

        def store(n0, n1, h0, h1):
            chunk, j0 = divmod(n0, CHUNK)
            b, t0 = divmod(n0, TOK)
            toks = slice(t0, t0 + n1 - n0)
            for view, first, last in (
                (q_view, 0, Q_HEADS), (k_view, Q_HEADS, ROPED_HEADS), (v_view, ROPED_HEADS, HEADS)
            ):
                a, z = max(h0, first), min(h1, last)
                if a < z:
                    nc.sync.dma_start(
                        out=view[b, :, a - first : z - first, toks, :],
                        in_=out_tiles[chunk][:, a:z, j0 : j0 + n1 - n0, :],
                    )

        def finish(n):
            if n < TILES - 1:
                bounds = (0, BANK_HEADS, ROPED_HEADS) if n == TILES - GROUP else (0, ROPED_HEADS)
                for h0, h1 in zip(bounds, bounds[1:]):
                    add_partners(nc.gpsimd, n, h0, h1)
                size = CHUNK if n < TILES - 2 * CHUNK else GROUP
                if n % size == size - 1:
                    store(n - size + 1, n + 1, 0, HEADS)
            else:
                store(n - GROUP + 1, n + 1, ROPED_HEADS, HEADS)
                for h0, h1 in ((Q_HEADS, ROPED_HEADS), (0, BANK_HEADS), (BANK_HEADS, Q_HEADS)):
                    add_partners(nc.vector, n, h0, h1)
                    store(n - GROUP + 1, n + 1, h0, h1)

        def exists(n):
            return 0 <= n < TILES

        w_jobs = {
            -4: ((group_w, 0, 0), (group_w, 0, 1), (quantise_w, 0, 0), (quantise_w, 0, 1)),
            -3: ((group_w, 1, 0),),
            -2: ((group_w, 1, 1), (quantise_w, 1, 0), (quantise_w, 1, 1)),
            -1: ((group_w, 2, 0), (group_w, 2, 1), (quantise_w, 2, 0), (quantise_w, 2, 1)),
        }

        with tc.manual_schedule():
            make_gain_diag()
            for step in range(-4, TILES):
                odd = step % GROUP == 1
                if odd and exists(step):
                    rope_k_straight(step // GROUP)
                if odd and exists(step):
                    rope_k_cross(step // GROUP)
                    finish(step - 1)
                if exists(step + 1):
                    quantise_x(step + 1)
                if exists(step + 4):
                    transpose_raw(step + 4)
                if exists(step + 2):
                    transpose_words(step + 2)
                if exists(step + 3):
                    multiply_gain(step + 3, 0)
                    multiply_gain(step + 3, 1)
                if step == 0:
                    multiply(0, 1)
                    multiply(0, 2)
                if exists(step + 4):
                    square(step + 4)
                if exists(step + 4):
                    copy_raw(step + 4)
                if exists(step):
                    rope_q(step, 0)
                if exists(step + 2):
                    group_x(step + 2)
                if exists(step + 1) and step >= 0:
                    multiply(step + 1, 2)
                if exists(step + 1):
                    multiply(step + 1, 0)
                if exists(step + 3):
                    scale(step + 3, 0)
                if not odd and exists(step + 1):
                    copy_v((step + 1) // GROUP)
                if exists(step + 3):
                    scale(step + 3, 1)
                for job, part, c in w_jobs.get(step, ()):
                    job(part, c)
                if step == -1:
                    make_rope_tables()
                if exists(step):
                    rope_q(step, 1)
                if exists(step + 1) and step >= 0:
                    multiply(step + 1, 1)
                if odd and exists(step):
                    finish(step)
